import numpy as np
import ml_dtypes


def mxq(x, axis, fmt="e4m3"):
    dtype, down = {"e4m3": (ml_dtypes.float8_e4m3fn, 7), "e5m2": (ml_dtypes.float8_e5m2, 14)}[fmt]
    v = np.moveaxis(np.asarray(x, np.float32).astype(ml_dtypes.bfloat16).astype(np.float64), axis, -1)
    blocks = v.reshape(v.shape[:-1] + (-1, 32))
    amax = np.abs(blocks).max(-1, keepdims=True)
    byte = np.maximum(np.where(amax > 0, np.frexp(amax)[1] - 1 + 127, 0) - down, 1)
    scale = np.exp2(byte - 127.0)
    codes = (blocks / scale).astype(np.float32).astype(dtype).astype(np.float64)
    return np.moveaxis((codes * scale).reshape(v.shape), -1, axis)


WIDE = False


def mx_kscale(k):
    if not WIDE:
        return np.ones(k)
    levels = np.array([10, -10, 5, -5, 0])
    if k % 512:
        return np.exp2(np.random.permutation(np.resize(levels, k // 32))).repeat(32)
    a = np.empty((k // 512, 16))
    for p in range(k // 512):
        a[p, :8] = np.random.permutation(np.resize(levels, 8))
        for g in range(8):
            far = levels[np.abs(levels - a[p, g]) >= 10]
            a[p, g + 8] = far[np.random.randint(len(far))]
    return np.exp2(a.ravel()).repeat(32)


BF16 = ml_dtypes.bfloat16


def bf(x):
    return np.asarray(x, np.float32).astype(BF16)


def f64(x):
    return np.asarray(x).astype(np.float64)


B, F, D = 256, 128, 24
K = F * D
LN_EPS = 1e-5


def layernorm(x, w, b):
    mu = x.mean(-1, keepdims=True)
    var = ((x - mu) ** 2).mean(-1, keepdims=True)
    return (x - mu) / np.sqrt(var + LN_EPS) * w + b


def setup_inputs():
    s = mx_kscale(K)
    sf = s.reshape(F, D)
    a = np.random.standard_normal((B, F, D))
    c = np.random.standard_normal((B, F, D))
    return {"r": bf(np.random.standard_normal((B, F, D)) * sf),
            "p": bf(np.random.standard_normal((B, F, D)) * sf),
            "log_lam": bf(0.5 * np.log(a ** 2 + c ** 2 + 1e-8)),
            "theta": bf(np.random.uniform(-np.pi, np.pi, (B, F, D))),
            "inter_orders": bf(np.random.standard_normal((F, F)) / np.sqrt(F)),
            "im_w": bf(np.random.standard_normal((K, K)) / np.sqrt(K) / s[:, None]),
            "im_b": bf(np.random.standard_normal(K) * 0.3),
            "bias_lam": bf(np.random.standard_normal((1, D, F)) * 0.3),
            "bias_theta": bf(np.random.standard_normal((1, D, F)) * 0.3),
            "norm_r_w": bf(1.0 + 0.2 * np.random.standard_normal(D)),
            "norm_r_b": bf(0.2 * np.random.standard_normal(D)),
            "norm_p_w": bf(1.0 + 0.2 * np.random.standard_normal(D)),
            "norm_p_b": bf(0.2 * np.random.standard_normal(D))}


def reference(r, p, log_lam, theta, inter_orders, im_w, im_b, bias_lam, bias_theta, norm_r_w, norm_r_b, norm_p_w, norm_p_b):
    io = f64(inter_orders)
    lam_t = np.swapaxes(f64(log_lam), -2, -1) @ io + f64(bias_lam)
    theta_t = np.swapaxes(f64(theta), -2, -1) @ io + f64(bias_theta)
    lam = np.swapaxes(np.exp(lam_t), -2, -1)
    th = np.swapaxes(theta_t, -2, -1)
    wq = mxq(f64(im_w), 0, "e4m3")
    r_lin = np.maximum((mxq(f64(r).reshape(B, K), 1, "e4m3") @ wq) + f64(im_b), 0.0).reshape(B, F, D)
    p_lin = np.maximum((mxq(f64(p).reshape(B, K), 1, "e4m3") @ wq) + f64(im_b), 0.0).reshape(B, F, D)
    o_r = r_lin + lam * np.cos(th)
    o_p = p_lin + lam * np.sin(th)
    return (layernorm(o_r, f64(norm_r_w), f64(norm_r_b)), layernorm(o_p, f64(norm_p_w), f64(norm_p_b)))

@@ -1,0 +1,360 @@
+import math
+
+import concourse.mybir as mybir
+from concourse.masks import make_identity
+
+F32 = mybir.dt.float32
+BF16 = mybir.dt.bfloat16
+U32 = mybir.dt.uint32
+U8 = mybir.dt.uint8
+FP8X4 = mybir.dt.float8_e4m3fn_x4
+ACT = mybir.ActivationFunctionType
+ALU = mybir.AluOpType
+AXIS_X = mybir.AxisListType.X
+
+P = 128
+BATCH = 256
+FIELDS = 128
+EMB = 24
+K = FIELDS * EMB
+B_TILES = BATCH // P
+M_TILES = 2 * B_TILES
+K_PASS = 512
+PASSES = K // K_PASS
+HALF = K_PASS // 2
+ROUND_FIELDS = 16
+ROUND_COLS = ROUND_FIELDS * EMB
+ROUNDS = FIELDS // ROUND_FIELDS
+WIDE = 256
+QUAD = 4
+ROUND_BLOCKS = ROUND_COLS // P
+POLAR_PIECES = 2
+LN_EPS = 1e-5
+ROUNDS_AHEAD = 4
+LOADS_AHEAD = 8
+VECTOR_ROUNDS = 3
+ROUND_MAGIC = 12582912.0
+
+FLOPS = 2 * (2 * BATCH) * K * K + 2 * 2 * BATCH * EMB * FIELDS * FIELDS
+
+
+def tile_eulerinteractionlayer_pa_kernel(
+    tc,
+    r,
+    p,
+    log_lam,
+    theta,
+    inter_orders,
+    im_w,
+    im_b,
+    bias_lam,
+    bias_theta,
+    norm_r_w,
+    norm_r_b,
+    norm_p_w,
+    norm_p_b,
+    out_0,
+    out_1,
+):
+    nc = tc.nc
+    with (
+        tc.tile_pool(name="keep", bufs=1) as keep,
+        tc.tile_pool(name="w_raw", bufs=LOADS_AHEAD) as w_raw_pool,
+        tc.tile_pool(name="w_grouped", bufs=PASSES) as w_grouped_pool,
+        tc.tile_pool(name="w_mx", bufs=ROUNDS_AHEAD * PASSES) as w_mx_pool,
+        tc.psum_pool(name="acc", bufs=M_TILES) as acc_pool,
+        tc.psum_pool(name="aux", bufs=4) as aux_pool,
+    ):
+        ident_f32 = keep.tile([P, P], F32)
+        make_identity(nc, ident_f32[:])
+        ones_bf = keep.tile([P, P], BF16)
+        nc.vector.memset(ones_bf[:], 1.0)
+        eps = keep.tile([P, 1], F32)
+        nc.vector.memset(eps[:], LN_EPS)
+        orders = keep.tile([P, FIELDS], BF16)
+        nc.sync.dma_start(out=orders[:], in_=inter_orders)
+
+        a_codes = keep.tile([P, M_TILES, PASSES, P], U32, align_bytes=64)
+        a_scales = keep.tile([P, M_TILES, PASSES, P], U8, align_bytes=64)
+        neg_polar = keep.tile([P, M_TILES, K], F32)
+        imb_all = keep.tile([P, K], BF16)
+        gain_col = keep.tile([P, ROUND_BLOCKS, 2], F32)
+        bias_col = keep.tile([P, ROUND_BLOCKS, 2], F32)
+
+        w_raw_tiles = {}
+
+        def load_chunk(chunk):
+            rnd, c = divmod(chunk, PASSES)
+            cols = slice(rnd * ROUND_COLS, (rnd + 1) * ROUND_COLS)
+            w_raw = w_raw_pool.tile([P, 4, ROUND_COLS], BF16)
+            nc.sync.dma_start(
+                out=w_raw[:],
+                in_=im_w[c * K_PASS : (c + 1) * K_PASS, cols].rearrange("(q t) n -> q t n", t=4),
+            )
+            w_raw_tiles[chunk] = w_raw
+
+        def quantise_chunk(chunk):
+            w_raw = w_raw_tiles.pop(chunk)
+            w_grouped = w_grouped_pool.tile([P, ROUND_COLS, 4], BF16, align_bytes=64)
+            regroup = nc.vector.tensor_copy if chunk < VECTOR_ROUNDS * PASSES else nc.scalar.copy
+            regroup(
+                out=w_grouped[:].rearrange("q (n i) t -> q n t i", i=4),
+                in_=w_raw[:].rearrange("q t (n i) -> q n t i", i=4),
+            )
+            codes = w_mx_pool.tile([P, ROUND_COLS], U32, align_bytes=64)
+            scales = w_mx_pool.tile([P, ROUND_COLS], U8, align_bytes=64)
+            for lo, hi in ((0, WIDE), (WIDE, ROUND_COLS)):
+                nc.vector.quantize_mx(
+                    out=codes[:, lo:hi].bitcast(FP8X4),
+                    scales=scales[:, lo:hi],
+                    in_=w_grouped[:, lo:hi, :].rearrange("q n t -> q (n t)"),
+                )
+            return codes, scales
+
+        with tc.tile_pool(name="head", bufs=1) as head:
+            bias_rows = head.tile([P, 2, K], BF16)
+            nc.gpsimd.memset(bias_rows[:], 0.0)
+            polar_inputs = ((theta, bias_theta), (log_lam, bias_lam))
+            raws = {}
+            for kind, (x, bias) in enumerate(polar_inputs):
+                nc.sync.dma_start(
+                    out=bias_rows[0:1, kind, :], in_=bias.rearrange("o d g -> o (d g)")
+                )
+                for bt in range(B_TILES):
+                    raw = head.tile([P, K], BF16, tag="raw", bufs=3)
+                    nc.sync.dma_start(
+                        out=raw[:],
+                        in_=x.rearrange("b f d -> b (f d)")[bt * P : (bt + 1) * P, :],
+                    )
+                    raws[kind, bt] = raw
+            for chunk in range(LOADS_AHEAD):
+                load_chunk(chunk)
+
+            for kind in range(2):
+                for bt in range(B_TILES):
+                    by_word = head.tile([P, EMB // 2, FIELDS], F32)
+                    words = raws[kind, bt][:].bitcast(F32).rearrange("b (f w) -> b w f", w=EMB // 2)
+                    x_t = head.tile([P, EMB // 2, P, 2], BF16, bufs=2)
+                    x_t_words = x_t[:].bitcast(F32)
+                    for w0 in range(0, EMB // 2, QUAD):
+                        nc.vector.tensor_copy(
+                            out=by_word[:, w0 : w0 + QUAD, :], in_=words[:, w0 : w0 + QUAD, :]
+                        )
+                        flipped = aux_pool.tile([P, QUAD, P], F32, tag="aux")
+                        for i in range(QUAD):
+                            nc.tensor.transpose(flipped[:, i, :], by_word[:, w0 + i, :], ident_f32[:])
+                        nc.scalar.copy(out=x_t_words[:, w0 : w0 + QUAD, :, 0], in_=flipped[:])
+                    for d0 in range(0, EMB, QUAD):
+                        mixed = aux_pool.tile([P, QUAD, FIELDS], F32, tag="aux")
+                        for i in range(QUAD):
+                            d = d0 + i
+                            nc.tensor.matmul(
+                                mixed[:, i, :],
+                                lhsT=ones_bf[:],
+                                rhs=bias_rows[:, kind, d * FIELDS : (d + 1) * FIELDS],
+                                start=True,
+                                stop=False,
+                            )
+                            nc.tensor.matmul(
+                                mixed[:, i, :],
+                                lhsT=x_t[:, d // 2, :, d % 2],
+                                rhs=orders[:],
+                                start=False,
+                                stop=True,
+                            )
+                        by_field = mixed[:].rearrange("b i g -> b g i")
+                        if kind == 0:
+                            nc.scalar.activation(
+                                out=neg_polar[:, B_TILES + bt, :].rearrange(
+                                    "b (g d) -> b g d", d=EMB
+                                )[:, :, d0 : d0 + QUAD],
+                                in_=by_field,
+                                func=ACT.Copy,
+                                scale=1.0 / (2.0 * math.pi),
+                            )
+                        else:
+                            nc.scalar.activation(
+                                out=neg_polar[:, bt, :].rearrange("b (g d) -> b g d", d=EMB)[
+                                    :, :, d0 : d0 + QUAD
+                                ],
+                                in_=by_field,
+                                func=ACT.Exp,
+                            )
+            for bt in range(B_TILES):
+                for piece in range(POLAR_PIECES):
+                    span = slice(piece * K // POLAR_PIECES, (piece + 1) * K // POLAR_PIECES)
+                    lam = neg_polar[:, bt, span]
+                    turns = neg_polar[:, B_TILES + bt, span]
+                    part = head.tile([P, K // POLAR_PIECES], F32, bufs=3)
+                    nc.vector.tensor_scalar(
+                        out=part[:],
+                        in0=turns,
+                        scalar1=ROUND_MAGIC,
+                        scalar2=ROUND_MAGIC,
+                        op0=ALU.add,
+                        op1=ALU.subtract,
+                    )
+                    nc.vector.tensor_tensor(out=part[:], in0=part[:], in1=turns, op=ALU.subtract)
+                    nc.scalar.activation(out=turns, in_=part[:], func=ACT.Sin, scale=2.0 * math.pi)
+                    nc.scalar.activation(out=part[:], in_=part[:], func=ACT.Sin, scale=math.pi)
+                    nc.scalar.activation(
+                        out=part[:], in_=part[:], func=ACT.Square, scale=math.sqrt(2.0)
+                    )
+                    nc.vector.tensor_tensor(out=turns, in0=turns, in1=lam, op=ALU.mult)
+                    nc.vector.scalar_tensor_tensor(
+                        out=lam, in0=part[:], scalar=1.0, in1=lam, op0=ALU.subtract, op1=ALU.mult
+                    )
+
+            for m in range(M_TILES):
+                source = r if m < B_TILES else p
+                rows = slice((m % B_TILES) * P, (m % B_TILES + 1) * P)
+                raw = head.tile([P, K], BF16, tag="raw", bufs=3)
+                nc.sync.dma_start(out=raw[:], in_=source.rearrange("b f d -> b (f d)")[rows, :])
+                raw_words = raw[:].bitcast(F32)
+                a_grouped = head.tile([P, PASSES, P, 4], BF16, align_bytes=64)
+                a_grouped_words = a_grouped[:].bitcast(F32)
+                for c0 in range(0, PASSES, 2):
+                    flipped = aux_pool.tile([P, 2, 2, P], F32, tag="aux")
+                    for j in range(2):
+                        for u in range(2):
+                            first = (c0 + j) * HALF + u
+                            nc.tensor.transpose(
+                                flipped[:, j, u, :],
+                                raw_words[:, first : (c0 + j + 1) * HALF : 2],
+                                ident_f32[:],
+                            )
+                    nc.vector.tensor_copy(
+                        out=a_grouped_words[:, c0 : c0 + 2, :, :],
+                        in_=flipped[:].rearrange("q j u b -> q j b u"),
+                    )
+                for lo, hi in ((0, 4), (4, 6)):
+                    nc.vector.quantize_mx(
+                        out=a_codes[:, m, lo:hi, :].rearrange("q c b -> q (c b)").bitcast(FP8X4),
+                        scales=a_scales[:, m, lo:hi, :].rearrange("q c b -> q (c b)"),
+                        in_=a_grouped[:, lo:hi, :, :].rearrange("q c b t -> q (c b t)"),
+                    )
+
+            nc.sync.dma_start(out=imb_all[:], in_=im_b.partition_broadcast(P))
+            for vec, dest, t in (
+                (norm_r_w, gain_col, 0),
+                (norm_p_w, gain_col, 1),
+                (norm_r_b, bias_col, 0),
+                (norm_p_b, bias_col, 1),
+            ):
+                spread = head.tile([P, EMB], BF16, bufs=4)
+                nc.sync.dma_start(out=spread[:], in_=vec.partition_broadcast(P))
+                equal_rows = head.tile([P, ROUND_FIELDS, EMB], F32)
+                nc.vector.tensor_copy(
+                    out=equal_rows[:],
+                    in_=spread[:].unsqueeze(1).to_broadcast([P, ROUND_FIELDS, EMB]),
+                )
+                flipped = aux_pool.tile([P, ROUND_BLOCKS, P], F32, tag="aux")
+                for block in range(ROUND_BLOCKS):
+                    nc.tensor.transpose(
+                        flipped[:, block, :],
+                        equal_rows[:].rearrange("b g d -> b (g d)")[:, block * P : (block + 1) * P],
+                        ident_f32[:],
+                    )
+                nc.vector.tensor_copy(out=dest[:, :, t], in_=flipped[:, :, 0])
+
+        with tc.tile_pool(name="tail", bufs=2) as tail:
+            for rnd in range(ROUNDS):
+                cols = slice(rnd * ROUND_COLS, (rnd + 1) * ROUND_COLS)
+                w_codes = []
+                w_scales = []
+                for c in range(PASSES):
+                    chunk = rnd * PASSES + c
+                    codes, scales = quantise_chunk(chunk)
+                    w_codes.append(codes)
+                    w_scales.append(scales)
+                    if chunk + LOADS_AHEAD < ROUNDS * PASSES:
+                        load_chunk(chunk + LOADS_AHEAD)
+
+                biased = tail.tile([P, M_TILES, ROUND_COLS], F32)
+                for m in range(M_TILES):
+                    acc = acc_pool.tile([P, ROUND_COLS], F32)
+                    for lo, hi in ((0, WIDE), (WIDE, ROUND_COLS)):
+                        for c in range(PASSES):
+                            nc.tensor.matmul_mx(
+                                out=acc[:, lo:hi],
+                                lhsT=a_codes[:, m, c, :].bitcast(FP8X4),
+                                lhsT_scale=a_scales[:, m, c, :],
+                                rhs=w_codes[c][:, lo:hi].bitcast(FP8X4),
+                                rhs_scale=w_scales[c][:, lo:hi],
+                                start=(c == 0),
+                                stop=(c == PASSES - 1),
+                            )
+                    nc.vector.tensor_tensor(
+                        out=biased[:, m, :], in0=acc[:], in1=imb_all[:, cols], op=ALU.add
+                    )
+                groups = M_TILES * ROUND_FIELDS
+                o = tail.tile([P, M_TILES, ROUND_COLS], F32)
+                nc.vector.scalar_tensor_tensor(
+                    out=o[:],
+                    in0=biased[:],
+                    scalar=0.0,
+                    in1=neg_polar[:, :, cols],
+                    op0=ALU.max,
+                    op1=ALU.subtract,
+                )
+                o_groups = o[:].rearrange("b m (g d) -> b (m g) d", d=EMB)
+                total = tail.tile([P, groups], F32)
+                nc.vector.tensor_reduce(out=total[:], in_=o_groups, axis=AXIS_X, op=ALU.add)
+                centred = tail.tile([P, groups, EMB], F32)
+                nc.vector.scalar_tensor_tensor(
+                    out=centred[:],
+                    in0=total[:].unsqueeze(2).to_broadcast([P, groups, EMB]),
+                    scalar=-1.0 / EMB,
+                    in1=o_groups,
+                    op0=ALU.mult,
+                    op1=ALU.add,
+                )
+                squares = tail.tile([P, groups, EMB], F32)
+                nc.scalar.activation(out=squares[:], in_=centred[:], func=ACT.Square)
+                spread2 = tail.tile([P, groups], F32)
+                nc.vector.tensor_reduce(out=spread2[:], in_=squares[:], axis=AXIS_X, op=ALU.add)
+                rstd = tail.tile([P, groups], F32)
+                nc.scalar.activation(
+                    out=rstd[:],
+                    in_=spread2[:],
+                    func=ACT.Abs_reciprocal_sqrt,
+                    scale=1.0 / EMB,
+                    bias=eps[:, 0:1],
+                )
+                nc.vector.tensor_tensor(
+                    out=centred[:],
+                    in0=centred[:],
+                    in1=rstd[:].unsqueeze(2).to_broadcast([P, groups, EMB]),
+                    op=ALU.mult,
+                )
+                normed = centred[:].rearrange("b (m g) d -> b m (g d)", m=M_TILES)
+                y_t = tail.tile([P, ROUND_BLOCKS, M_TILES, P], F32)
+                for block in range(ROUND_BLOCKS):
+                    flipped = aux_pool.tile([P, M_TILES, P], F32, tag="aux")
+                    for m in range(M_TILES):
+                        nc.tensor.transpose(
+                            flipped[:, m, :], normed[:, m, block * P : (block + 1) * P], ident_f32[:]
+                        )
+                    for t in range(2):
+                        tiles = slice(t * B_TILES, (t + 1) * B_TILES)
+                        nc.scalar.activation(
+                            out=y_t[:, block, tiles, :],
+                            in_=flipped[:, tiles, :],
+                            func=ACT.Identity,
+                            scale=gain_col[:, block, t : t + 1],
+                            bias=bias_col[:, block, t : t + 1],
+                        )
+                y = tail.tile([P, M_TILES * ROUND_BLOCKS, P], F32)
+                for j0 in range(0, M_TILES * ROUND_BLOCKS, QUAD):
+                    back = aux_pool.tile([P, QUAD, P], F32, tag="aux")
+                    for i in range(QUAD):
+                        m, block = divmod(j0 + i, ROUND_BLOCKS)
+                        nc.tensor.transpose(back[:, i, :], y_t[:, block, m, :], ident_f32[:])
+                    nc.scalar.copy(out=y[:, j0 : j0 + QUAD, :], in_=back[:])
+                for dest, first in ((out_0, 0), (out_1, B_TILES)):
+                    nc.sync.dma_start(
+                        out=dest.rearrange("(t b) f d -> b t (f d)", t=B_TILES)[:, :, cols],
+                        in_=y[:].rearrange("b (m k) n -> b m (k n)", m=M_TILES)[
+                            :, first : first + B_TILES, :
+                        ],
+                    )

@@ -17,23 +17,27 @@ BATCH = 256
 FIELDS = 128
 EMB = 24
 K = FIELDS * EMB
-B_TILES = BATCH // P
-M_TILES = 2 * B_TILES
+SIDES = 2
+M_TILES = 4
+SAMPLES = SIDES * BATCH
 K_PASS = 512
 PASSES = K // K_PASS
 HALF = K_PASS // 2
-ROUND_FIELDS = 16
+ROUND_FIELDS = 32
 ROUND_COLS = ROUND_FIELDS * EMB
 ROUNDS = FIELDS // ROUND_FIELDS
-WIDE = 256
-QUAD = 4
-ROUND_BLOCKS = ROUND_COLS // P
-POLAR_PIECES = 2
+VALS = 4
+BLOCKS = EMB // VALS
+STEPS = ROUNDS * BLOCKS
+THIRD = 2
+THIRDS = PASSES // THIRD
 LN_EPS = 1e-5
-ROUNDS_AHEAD = 4
-LOADS_AHEAD = 8
-VECTOR_ROUNDS = 3
+PREP_AHEAD = 4
 ROUND_MAGIC = 12582912.0
+ROW_BIAS = 0
+ROW_CENTRED = 32
+ROW_GAIN = 64
+ROW_SHIFT = 66
 
 FLOPS = 2 * (2 * BATCH) * K * K + 2 * 2 * BATCH * EMB * FIELDS * FIELDS
 
@@ -57,304 +61,413 @@ def tile_eulerinteractionlayer_pa_kernel(
     out_1,
 ):
     nc = tc.nc
+    outs = (out_0, out_1)
+    flat = [o.rearrange("b f d -> (b f d)") for o in outs]
+    park = [x.rearrange("(j g n) -> j g n", j=BLOCKS, g=FIELDS) for x in flat]
+    unpark = [x.rearrange("(j r q b) -> j q r b", j=BLOCKS, r=ROUNDS, q=P) for x in flat]
     with (
         tc.tile_pool(name="keep", bufs=1) as keep,
-        tc.tile_pool(name="w_raw", bufs=LOADS_AHEAD) as w_raw_pool,
-        tc.tile_pool(name="w_grouped", bufs=PASSES) as w_grouped_pool,
-        tc.tile_pool(name="w_mx", bufs=ROUNDS_AHEAD * PASSES) as w_mx_pool,
-        tc.psum_pool(name="acc", bufs=M_TILES) as acc_pool,
-        tc.psum_pool(name="aux", bufs=4) as aux_pool,
+        tc.tile_pool(name="w_raw", bufs=5) as w_raw_pool,
+        tc.tile_pool(name="w_grouped", bufs=3) as w_grouped_pool,
+        tc.tile_pool(name="w_mx", bufs=PREP_AHEAD + 2) as w_mx_pool,
+        tc.psum_pool(name="acc", bufs=3) as acc_pool,
+        tc.psum_pool(name="aux", bufs=5) as aux_pool,
     ):
-        ident_f32 = keep.tile([P, P], F32)
-        make_identity(nc, ident_f32[:])
-        ones_bf = keep.tile([P, P], BF16)
-        nc.vector.memset(ones_bf[:], 1.0)
+        ident = keep.tile([P, P], F32)
+        make_identity(nc, ident[:])
         eps = keep.tile([P, 1], F32)
         nc.vector.memset(eps[:], LN_EPS)
         orders = keep.tile([P, FIELDS], BF16)
         nc.sync.dma_start(out=orders[:], in_=inter_orders)
 
-        a_codes = keep.tile([P, M_TILES, PASSES, P], U32, align_bytes=64)
-        a_scales = keep.tile([P, M_TILES, PASSES, P], U8, align_bytes=64)
-        neg_polar = keep.tile([P, M_TILES, K], F32)
-        imb_all = keep.tile([P, K], BF16)
-        gain_col = keep.tile([P, ROUND_BLOCKS, 2], F32)
-        bias_col = keep.tile([P, ROUND_BLOCKS, 2], F32)
+        a_codes = keep.tile([P, PASSES, SAMPLES], U32, align_bytes=64)
+        a_scales = keep.tile([P, PASSES, SAMPLES], U8, align_bytes=64)
+        neg_polar = keep.tile([P, BLOCKS, ROUNDS, SAMPLES], F32)
+        cols = keep.tile([P, BLOCKS, 68], F32)
+        neg_bias = keep.tile([P, BLOCKS, ROUNDS], F32)
+        shift_rows = keep.tile([P, BLOCKS, P], BF16)
+        ident_bf = keep.tile([P, P], BF16)
+        polar_bias = keep.tile([P, 2, EMB], F32)
 
-        w_raw_tiles = {}
+        w_raw = {}
 
-        def load_chunk(chunk):
-            rnd, c = divmod(chunk, PASSES)
-            cols = slice(rnd * ROUND_COLS, (rnd + 1) * ROUND_COLS)
-            w_raw = w_raw_pool.tile([P, 4, ROUND_COLS], BF16)
-            nc.sync.dma_start(
-                out=w_raw[:],
-                in_=im_w[c * K_PASS : (c + 1) * K_PASS, cols].rearrange("(q t) n -> q t n", t=4),
-            )
-            w_raw_tiles[chunk] = w_raw
+        def load_third(rnd, h):
+            tile = w_raw_pool.tile([P, THIRD, 4, ROUND_COLS], BF16, name="w_third")
+            for i in range(THIRD):
+                first = (h * THIRD + i) * K_PASS
+                nc.sync.dma_start(
+                    out=tile[:, i, :, :],
+                    in_=im_w[
+                        first : first + K_PASS, rnd * ROUND_COLS : (rnd + 1) * ROUND_COLS
+                    ].rearrange("(q t) n -> q t n", t=4),
+                )
+            w_raw[rnd, h] = tile
 
-        def quantise_chunk(chunk):
-            w_raw = w_raw_tiles.pop(chunk)
-            w_grouped = w_grouped_pool.tile([P, ROUND_COLS, 4], BF16, align_bytes=64)
-            regroup = nc.vector.tensor_copy if chunk < VECTOR_ROUNDS * PASSES else nc.scalar.copy
-            regroup(
-                out=w_grouped[:].rearrange("q (n i) t -> q n t i", i=4),
-                in_=w_raw[:].rearrange("q t (n i) -> q n t i", i=4),
-            )
-            codes = w_mx_pool.tile([P, ROUND_COLS], U32, align_bytes=64)
-            scales = w_mx_pool.tile([P, ROUND_COLS], U8, align_bytes=64)
-            for lo, hi in ((0, WIDE), (WIDE, ROUND_COLS)):
+        def prepare(step):
+            rnd, j = divmod(step, BLOCKS)
+            grouped = w_grouped_pool.tile([P, PASSES, P, 4], BF16, align_bytes=64)
+            for h in range(THIRDS):
+                if j == 0:
+                    load_third(rnd, h)
+                regroup = nc.scalar.copy if (step * THIRDS + h) % 2 else nc.vector.tensor_copy
+                regroup(
+                    out=grouped[:, h * THIRD : (h + 1) * THIRD, :, :].rearrange(
+                        "q c (g i) t -> q c g t i", i=VALS
+                    ),
+                    in_=w_raw[rnd, h][:].rearrange("q c t (g j i) -> q j c g t i", j=BLOCKS, i=VALS)[
+                        :, j
+                    ],
+                )
+            codes = w_mx_pool.tile([P, PASSES, P], U32, align_bytes=64)
+            scales = w_mx_pool.tile([P, PASSES, P], U8, align_bytes=64)
+            for lo, hi in ((0, 4), (4, 6)):
                 nc.vector.quantize_mx(
-                    out=codes[:, lo:hi].bitcast(FP8X4),
-                    scales=scales[:, lo:hi],
-                    in_=w_grouped[:, lo:hi, :].rearrange("q n t -> q (n t)"),
+                    out=codes[:, lo:hi, :].rearrange("q c n -> q (c n)").bitcast(FP8X4),
+                    scales=scales[:, lo:hi, :].rearrange("q c n -> q (c n)"),
+                    in_=grouped[:, lo:hi, :, :].rearrange("q c n t -> q (c n t)"),
                 )
             return codes, scales
 
         with tc.tile_pool(name="head", bufs=1) as head:
-            bias_rows = head.tile([P, 2, K], BF16)
-            nc.gpsimd.memset(bias_rows[:], 0.0)
-            polar_inputs = ((theta, bias_theta), (log_lam, bias_lam))
-            raws = {}
-            for kind, (x, bias) in enumerate(polar_inputs):
-                nc.sync.dma_start(
-                    out=bias_rows[0:1, kind, :], in_=bias.rearrange("o d g -> o (d g)")
-                )
-                for bt in range(B_TILES):
-                    raw = head.tile([P, K], BF16, tag="raw", bufs=3)
+            polar_rows = head.tile([P, P], BF16)
+            nc.gpsimd.memset(polar_rows[:], 0.0)
+            nc.sync.dma_start(out=polar_rows[0:EMB, :], in_=bias_theta.rearrange("o d g -> (o d) g"))
+            nc.sync.dma_start(
+                out=polar_rows[32 : 32 + EMB, :], in_=bias_lam.rearrange("o d g -> (o d) g")
+            )
+
+            def load_rows(x):
+                tiles = []
+                for bt in range(2):
+                    raw = head.tile([P, K], BF16, tag="raw", bufs=4)
                     nc.sync.dma_start(
                         out=raw[:],
                         in_=x.rearrange("b f d -> b (f d)")[bt * P : (bt + 1) * P, :],
                     )
-                    raws[kind, bt] = raw
-            for chunk in range(LOADS_AHEAD):
-                load_chunk(chunk)
+                    tiles.append(raw)
+                return tiles
 
-            for kind in range(2):
-                for bt in range(B_TILES):
-                    by_word = head.tile([P, EMB // 2, FIELDS], F32)
-                    words = raws[kind, bt][:].bitcast(F32).rearrange("b (f w) -> b w f", w=EMB // 2)
-                    x_t = head.tile([P, EMB // 2, P, 2], BF16, bufs=2)
-                    x_t_words = x_t[:].bitcast(F32)
-                    for w0 in range(0, EMB // 2, QUAD):
-                        nc.vector.tensor_copy(
-                            out=by_word[:, w0 : w0 + QUAD, :], in_=words[:, w0 : w0 + QUAD, :]
-                        )
-                        flipped = aux_pool.tile([P, QUAD, P], F32, tag="aux")
-                        for i in range(QUAD):
-                            nc.tensor.transpose(flipped[:, i, :], by_word[:, w0 + i, :], ident_f32[:])
-                        nc.scalar.copy(out=x_t_words[:, w0 : w0 + QUAD, :, 0], in_=flipped[:])
-                    for d0 in range(0, EMB, QUAD):
-                        mixed = aux_pool.tile([P, QUAD, FIELDS], F32, tag="aux")
-                        for i in range(QUAD):
-                            d = d0 + i
-                            nc.tensor.matmul(
-                                mixed[:, i, :],
-                                lhsT=ones_bf[:],
-                                rhs=bias_rows[:, kind, d * FIELDS : (d + 1) * FIELDS],
-                                start=True,
-                                stop=False,
-                            )
-                            nc.tensor.matmul(
-                                mixed[:, i, :],
-                                lhsT=x_t[:, d // 2, :, d % 2],
-                                rhs=orders[:],
-                                start=False,
-                                stop=True,
-                            )
-                        by_field = mixed[:].rearrange("b i g -> b g i")
-                        if kind == 0:
-                            nc.scalar.activation(
-                                out=neg_polar[:, B_TILES + bt, :].rearrange(
-                                    "b (g d) -> b g d", d=EMB
-                                )[:, :, d0 : d0 + QUAD],
-                                in_=by_field,
-                                func=ACT.Copy,
-                                scale=1.0 / (2.0 * math.pi),
-                            )
-                        else:
-                            nc.scalar.activation(
-                                out=neg_polar[:, bt, :].rearrange("b (g d) -> b g d", d=EMB)[
-                                    :, :, d0 : d0 + QUAD
-                                ],
-                                in_=by_field,
-                                func=ACT.Exp,
-                            )
-            for bt in range(B_TILES):
-                for piece in range(POLAR_PIECES):
-                    span = slice(piece * K // POLAR_PIECES, (piece + 1) * K // POLAR_PIECES)
-                    lam = neg_polar[:, bt, span]
-                    turns = neg_polar[:, B_TILES + bt, span]
-                    part = head.tile([P, K // POLAR_PIECES], F32, bufs=3)
-                    nc.vector.tensor_scalar(
-                        out=part[:],
-                        in0=turns,
-                        scalar1=ROUND_MAGIC,
-                        scalar2=ROUND_MAGIC,
-                        op0=ALU.add,
-                        op1=ALU.subtract,
-                    )
-                    nc.vector.tensor_tensor(out=part[:], in0=part[:], in1=turns, op=ALU.subtract)
-                    nc.scalar.activation(out=turns, in_=part[:], func=ACT.Sin, scale=2.0 * math.pi)
-                    nc.scalar.activation(out=part[:], in_=part[:], func=ACT.Sin, scale=math.pi)
-                    nc.scalar.activation(
-                        out=part[:], in_=part[:], func=ACT.Square, scale=math.sqrt(2.0)
-                    )
-                    nc.vector.tensor_tensor(out=turns, in0=turns, in1=lam, op=ALU.mult)
-                    nc.vector.scalar_tensor_tensor(
-                        out=lam, in0=part[:], scalar=1.0, in1=lam, op0=ALU.subtract, op1=ALU.mult
-                    )
-
-            for m in range(M_TILES):
-                source = r if m < B_TILES else p
-                rows = slice((m % B_TILES) * P, (m % B_TILES + 1) * P)
-                raw = head.tile([P, K], BF16, tag="raw", bufs=3)
-                nc.sync.dma_start(out=raw[:], in_=source.rearrange("b f d -> b (f d)")[rows, :])
-                raw_words = raw[:].bitcast(F32)
-                a_grouped = head.tile([P, PASSES, P, 4], BF16, align_bytes=64)
-                a_grouped_words = a_grouped[:].bitcast(F32)
-                for c0 in range(0, PASSES, 2):
-                    flipped = aux_pool.tile([P, 2, 2, P], F32, tag="aux")
-                    for j in range(2):
-                        for u in range(2):
-                            first = (c0 + j) * HALF + u
-                            nc.tensor.transpose(
-                                flipped[:, j, u, :],
-                                raw_words[:, first : (c0 + j + 1) * HALF : 2],
-                                ident_f32[:],
-                            )
-                    nc.vector.tensor_copy(
-                        out=a_grouped_words[:, c0 : c0 + 2, :, :],
-                        in_=flipped[:].rearrange("q j u b -> q j b u"),
-                    )
-                for lo, hi in ((0, 4), (4, 6)):
-                    nc.vector.quantize_mx(
-                        out=a_codes[:, m, lo:hi, :].rearrange("q c b -> q (c b)").bitcast(FP8X4),
-                        scales=a_scales[:, m, lo:hi, :].rearrange("q c b -> q (c b)"),
-                        in_=a_grouped[:, lo:hi, :, :].rearrange("q c b t -> q (c b t)"),
-                    )
-
-            nc.sync.dma_start(out=imb_all[:], in_=im_b.partition_broadcast(P))
-            for vec, dest, t in (
-                (norm_r_w, gain_col, 0),
-                (norm_p_w, gain_col, 1),
-                (norm_r_b, bias_col, 0),
-                (norm_p_b, bias_col, 1),
-            ):
-                spread = head.tile([P, EMB], BF16, bufs=4)
-                nc.sync.dma_start(out=spread[:], in_=vec.partition_broadcast(P))
-                equal_rows = head.tile([P, ROUND_FIELDS, EMB], F32)
-                nc.vector.tensor_copy(
-                    out=equal_rows[:],
-                    in_=spread[:].unsqueeze(1).to_broadcast([P, ROUND_FIELDS, EMB]),
+            raw_lam = load_rows(log_lam)
+            raw_theta = load_rows(theta)
+            rows = head.tile([P, ROUND_FIELDS, EMB], BF16)
+            nc.gpsimd.memset(rows[:], 0.0)
+            for first in (ROW_BIAS, ROW_CENTRED):
+                nc.sync.dma_start(
+                    out=rows[first : first + ROUNDS, :, :],
+                    in_=im_b.rearrange("(r g d) -> r g d", r=ROUNDS, g=ROUND_FIELDS),
                 )
-                flipped = aux_pool.tile([P, ROUND_BLOCKS, P], F32, tag="aux")
-                for block in range(ROUND_BLOCKS):
-                    nc.tensor.transpose(
-                        flipped[:, block, :],
-                        equal_rows[:].rearrange("b g d -> b (g d)")[:, block * P : (block + 1) * P],
-                        ident_f32[:],
-                    )
-                nc.vector.tensor_copy(out=dest[:, :, t], in_=flipped[:, :, 0])
+            for row, vec in (
+                (ROW_GAIN, norm_r_w),
+                (ROW_GAIN + 1, norm_p_w),
+                (ROW_SHIFT, norm_r_b),
+                (ROW_SHIFT + 1, norm_p_b),
+            ):
+                nc.sync.dma_start(
+                    out=rows[row : row + 1, :, :],
+                    in_=vec.partition_broadcast(ROUND_FIELDS).unsqueeze(0),
+                )
 
-        with tc.tile_pool(name="tail", bufs=2) as tail:
-            for rnd in range(ROUNDS):
-                cols = slice(rnd * ROUND_COLS, (rnd + 1) * ROUND_COLS)
-                w_codes = []
-                w_scales = []
-                for c in range(PASSES):
-                    chunk = rnd * PASSES + c
-                    codes, scales = quantise_chunk(chunk)
-                    w_codes.append(codes)
-                    w_scales.append(scales)
-                    if chunk + LOADS_AHEAD < ROUNDS * PASSES:
-                        load_chunk(chunk + LOADS_AHEAD)
+            nc.vector.tensor_copy(out=ident_bf[:], in_=ident[:])
+            polar_rows_f32 = head.tile([P, P], F32)
+            nc.vector.tensor_copy(out=polar_rows_f32[:], in_=polar_rows[:])
+            flipped = aux_pool.tile([P, P], F32, tag="aux")
+            nc.tensor.transpose(flipped[:], polar_rows_f32[:], ident[:])
+            nc.scalar.activation(
+                out=polar_bias[:, 0, :],
+                in_=flipped[:, 0:EMB],
+                func=ACT.Copy,
+                scale=1.0 / (2.0 * math.pi),
+            )
+            nc.scalar.copy(out=polar_bias[:, 1, :], in_=flipped[:, 32 : 32 + EMB])
 
-                biased = tail.tile([P, M_TILES, ROUND_COLS], F32)
-                for m in range(M_TILES):
-                    acc = acc_pool.tile([P, ROUND_COLS], F32)
-                    for lo, hi in ((0, WIDE), (WIDE, ROUND_COLS)):
-                        for c in range(PASSES):
-                            nc.tensor.matmul_mx(
-                                out=acc[:, lo:hi],
-                                lhsT=a_codes[:, m, c, :].bitcast(FP8X4),
-                                lhsT_scale=a_scales[:, m, c, :],
-                                rhs=w_codes[c][:, lo:hi].bitcast(FP8X4),
-                                rhs_scale=w_scales[c][:, lo:hi],
-                                start=(c == 0),
-                                stop=(c == PASSES - 1),
-                            )
-                    nc.vector.tensor_tensor(
-                        out=biased[:, m, :], in0=acc[:], in1=imb_all[:, cols], op=ALU.add
-                    )
-                groups = M_TILES * ROUND_FIELDS
-                o = tail.tile([P, M_TILES, ROUND_COLS], F32)
-                nc.vector.scalar_tensor_tensor(
-                    out=o[:],
-                    in0=biased[:],
-                    scalar=0.0,
-                    in1=neg_polar[:, :, cols],
-                    op0=ALU.max,
+            def mix(raws, finish):
+                for w0 in range(0, EMB // 2, 4):
+                    x_t = head.tile([P, 4, BATCH, 2], BF16, bufs=2)
+                    x_t_words = x_t[:].bitcast(F32)
+                    for bt in range(2):
+                        by_word = head.tile([P, 4, FIELDS], F32, bufs=2)
+                        nc.vector.tensor_copy(
+                            out=by_word[:],
+                            in_=raws[bt][:].bitcast(F32).rearrange("b (f w) -> b w f", w=EMB // 2)[
+                                :, w0 : w0 + 4, :
+                            ],
+                        )
+                        flipped = aux_pool.tile([P, 4, P], F32, tag="aux")
+                        for i in range(4):
+                            nc.tensor.transpose(flipped[:, i, :], by_word[:, i, :], ident[:])
+                        nc.scalar.copy(
+                            out=x_t_words[:, :, bt * P : (bt + 1) * P, 0], in_=flipped[:]
+                        )
+                    for i in range(4):
+                        mixed = aux_pool.tile([P, BATCH, 2], F32, tag="aux")
+                        nc.tensor.matmul(
+                            mixed[:].rearrange("g b e -> g (b e)"),
+                            lhsT=orders[:],
+                            rhs=x_t[:, i, :, :].rearrange("f b e -> f (b e)"),
+                            start=True,
+                            stop=True,
+                        )
+                        for e in range(2):
+                            finish(2 * (w0 + i) + e, mixed[:, :, e])
+
+            held = neg_polar[:].rearrange("g j r s -> g j (r s)").rearrange(
+                "g j (t i b) -> g j t i b", t=2, i=VALS
+            )
+
+            def finish_lam(d, mixed):
+                nc.scalar.activation(
+                    out=held[:, d // VALS, 0, d % VALS, :],
+                    in_=mixed,
+                    func=ACT.Exp,
+                    bias=polar_bias[:, 1, d : d + 1],
+                )
+
+            def finish_theta(d, mixed):
+                nc.scalar.activation(
+                    out=held[:, d // VALS, 1, d % VALS, :],
+                    in_=mixed,
+                    func=ACT.Identity,
+                    scale=1.0 / (2.0 * math.pi),
+                    bias=polar_bias[:, 0, d : d + 1],
+                )
+
+            mix(raw_lam, finish_lam)
+            mix(raw_theta, finish_theta)
+            for j in range(BLOCKS):
+                lam = held[:, j, 0, :, :].rearrange("g i b -> g (i b)")
+                turns = held[:, j, 1, :, :].rearrange("g i b -> g (i b)")
+                part = head.tile([P, VALS * BATCH], F32, bufs=2)
+                nc.vector.tensor_scalar(
+                    out=part[:],
+                    in0=turns,
+                    scalar1=ROUND_MAGIC,
+                    scalar2=ROUND_MAGIC,
+                    op0=ALU.add,
                     op1=ALU.subtract,
                 )
-                o_groups = o[:].rearrange("b m (g d) -> b (m g) d", d=EMB)
-                total = tail.tile([P, groups], F32)
-                nc.vector.tensor_reduce(out=total[:], in_=o_groups, axis=AXIS_X, op=ALU.add)
-                centred = tail.tile([P, groups, EMB], F32)
+                nc.vector.tensor_tensor(out=part[:], in0=part[:], in1=turns, op=ALU.subtract)
+                neg_sin = head.tile([P, VALS * BATCH], F32, bufs=2)
+                nc.scalar.activation(out=neg_sin[:], in_=part[:], func=ACT.Sin, scale=2.0 * math.pi)
+                nc.scalar.activation(out=part[:], in_=part[:], func=ACT.Sin, scale=math.pi)
+                nc.scalar.activation(
+                    out=part[:], in_=part[:], func=ACT.Square, scale=math.sqrt(2.0)
+                )
+                nc.vector.tensor_tensor(out=neg_sin[:], in0=neg_sin[:], in1=lam, op=ALU.mult)
                 nc.vector.scalar_tensor_tensor(
-                    out=centred[:],
-                    in0=total[:].unsqueeze(2).to_broadcast([P, groups, EMB]),
+                    out=part[:], in0=part[:], scalar=1.0, in1=lam, op0=ALU.subtract, op1=ALU.mult
+                )
+                for side, term in ((0, part), (1, neg_sin)):
+                    nc.sync.dma_start(out=park[side][j], in_=term[:])
+            for j in range(BLOCKS):
+                for side in range(SIDES):
+                    nc.sync.dma_start(
+                        out=neg_polar[:, j, :, side * BATCH : (side + 1) * BATCH],
+                        in_=unpark[side][j],
+                    )
+
+            raw_x = load_rows(r) + load_rows(p)
+            for c in range(PASSES):
+                grouped = head.tile([P, SAMPLES, 4], BF16, align_bytes=64, bufs=2)
+                grouped_words = grouped[:].bitcast(F32)
+                for m0 in range(0, M_TILES, 2):
+                    flipped = aux_pool.tile([P, 2, 2, P], F32, tag="aux")
+                    for i in range(2):
+                        words = raw_x[m0 + i][:].bitcast(F32)
+                        for u in range(2):
+                            nc.tensor.transpose(
+                                flipped[:, i, u, :],
+                                words[:, c * HALF + u : (c + 1) * HALF : 2],
+                                ident[:],
+                            )
+                    nc.vector.tensor_copy(
+                        out=grouped_words[:, m0 * P : (m0 + 2) * P, :].rearrange(
+                            "q (i b) u -> q i b u", i=2
+                        ),
+                        in_=flipped[:].rearrange("q i u b -> q i b u"),
+                    )
+                nc.vector.quantize_mx(
+                    out=a_codes[:, c, :].bitcast(FP8X4),
+                    scales=a_scales[:, c, :],
+                    in_=grouped[:].rearrange("q n t -> q (n t)"),
+                )
+
+            nc.vector.tensor_copy(
+                out=shift_rows[:].rearrange("k j (g i) -> k j g i", i=VALS),
+                in_=rows[:].rearrange("k g (j i) -> k j g i", j=BLOCKS),
+            )
+            rows_f32 = head.tile([P, BLOCKS, P], F32)
+            nc.vector.tensor_copy(out=rows_f32[:], in_=shift_rows[:])
+            field_sum = head.tile([P, ROUND_FIELDS], F32)
+            nc.vector.tensor_reduce(out=field_sum[:], in_=rows[:], axis=AXIS_X, op=ALU.add)
+            centred_rows = rows_f32[32:64, :, :].rearrange("k j (g i) -> k j g i", i=VALS)
+            for j in range(BLOCKS):
+                nc.vector.scalar_tensor_tensor(
+                    out=centred_rows[:, j],
+                    in0=field_sum[32:64, :].unsqueeze(2).to_broadcast([32, ROUND_FIELDS, VALS]),
                     scalar=-1.0 / EMB,
-                    in1=o_groups,
+                    in1=centred_rows[:, j],
                     op0=ALU.mult,
                     op1=ALU.add,
                 )
-                squares = tail.tile([P, groups, EMB], F32)
-                nc.scalar.activation(out=squares[:], in_=centred[:], func=ACT.Square)
-                spread2 = tail.tile([P, groups], F32)
-                nc.vector.tensor_reduce(out=spread2[:], in_=squares[:], axis=AXIS_X, op=ALU.add)
-                rstd = tail.tile([P, groups], F32)
+            for j0 in range(0, BLOCKS, 3):
+                flipped = aux_pool.tile([P, 3, P], F32, tag="aux")
+                for i in range(3):
+                    nc.tensor.transpose(flipped[:, i, :], rows_f32[:, j0 + i, :], ident[:])
+                nc.scalar.copy(out=cols[:, j0 : j0 + 3, :], in_=flipped[:, :, 0:68])
+            nc.vector.tensor_scalar(
+                out=neg_bias[:],
+                in0=cols[:, :, ROW_BIAS : ROW_BIAS + ROUNDS],
+                scalar1=-1.0,
+                scalar2=None,
+                op0=ALU.mult,
+            )
+
+        with tc.tile_pool(name="tail", bufs=2) as tail:
+
+            def group_sums(x, side):
+                sums = aux_pool.tile([P, 2, P], F32, tag="aux")
+                for m in range(2):
+                    first = side * BATCH + m * P if x.shape[2] == SAMPLES else m * P
+                    for j in range(BLOCKS):
+                        nc.tensor.matmul(
+                            sums[:, m, :],
+                            lhsT=x[:, j, first : first + P],
+                            rhs=ident[:],
+                            is_transpose=True,
+                            start=(j == 0),
+                            stop=(j == BLOCKS - 1),
+                        )
+                total = tail.tile([P, 2 * ROUND_FIELDS], F32)
+                nc.vector.tensor_reduce(
+                    out=total[:],
+                    in_=sums[:].rearrange("b m (g i) -> b (m g) i", i=VALS),
+                    axis=AXIS_X,
+                    op=ALU.add,
+                )
+                return total
+
+            def spread(total, func, bias):
+                wide = tail.tile([P, 2 * ROUND_FIELDS, VALS], F32)
                 nc.scalar.activation(
-                    out=rstd[:],
-                    in_=spread2[:],
-                    func=ACT.Abs_reciprocal_sqrt,
+                    out=wide[:],
+                    in_=total[:].unsqueeze(2).to_broadcast([P, 2 * ROUND_FIELDS, VALS]),
+                    func=func,
                     scale=1.0 / EMB,
-                    bias=eps[:, 0:1],
+                    bias=bias,
                 )
-                nc.vector.tensor_tensor(
-                    out=centred[:],
-                    in0=centred[:],
-                    in1=rstd[:].unsqueeze(2).to_broadcast([P, groups, EMB]),
-                    op=ALU.mult,
-                )
-                normed = centred[:].rearrange("b (m g) d -> b m (g d)", m=M_TILES)
-                y_t = tail.tile([P, ROUND_BLOCKS, M_TILES, P], F32)
-                for block in range(ROUND_BLOCKS):
-                    flipped = aux_pool.tile([P, M_TILES, P], F32, tag="aux")
-                    for m in range(M_TILES):
-                        nc.tensor.transpose(
-                            flipped[:, m, :], normed[:, m, block * P : (block + 1) * P], ident_f32[:]
-                        )
-                    for t in range(2):
-                        tiles = slice(t * B_TILES, (t + 1) * B_TILES)
-                        nc.scalar.activation(
-                            out=y_t[:, block, tiles, :],
-                            in_=flipped[:, tiles, :],
-                            func=ACT.Identity,
-                            scale=gain_col[:, block, t : t + 1],
-                            bias=bias_col[:, block, t : t + 1],
-                        )
-                y = tail.tile([P, M_TILES * ROUND_BLOCKS, P], F32)
-                for j0 in range(0, M_TILES * ROUND_BLOCKS, QUAD):
-                    back = aux_pool.tile([P, QUAD, P], F32, tag="aux")
-                    for i in range(QUAD):
-                        m, block = divmod(j0 + i, ROUND_BLOCKS)
-                        nc.tensor.transpose(back[:, i, :], y_t[:, block, m, :], ident_f32[:])
-                    nc.scalar.copy(out=y[:, j0 : j0 + QUAD, :], in_=back[:])
-                for dest, first in ((out_0, 0), (out_1, B_TILES)):
-                    nc.sync.dma_start(
-                        out=dest.rearrange("(t b) f d -> b t (f d)", t=B_TILES)[:, :, cols],
-                        in_=y[:].rearrange("b (m k) n -> b m (k n)", m=M_TILES)[
-                            :, first : first + B_TILES, :
-                        ],
+                back = aux_pool.tile([P, 2, P], F32, tag="aux")
+                for m in range(2):
+                    nc.tensor.transpose(
+                        back[:, m, :],
+                        wide[:].rearrange("b (m g) i -> b m (g i)", m=2)[:, m, :],
+                        ident[:],
                     )
+                return back
+
+            def epilogue(rnd, side, o):
+                samples = slice(side * BATCH, (side + 1) * BATCH)
+                state = {}
+
+                def centre():
+                    back = spread(group_sums(o[:], side), ACT.Copy, 0.0)
+                    for j in range(BLOCKS):
+                        nc.vector.scalar_tensor_tensor(
+                            out=o[:, j, samples],
+                            in0=o[:, j, samples],
+                            scalar=cols[:, j, ROW_CENTRED + rnd : ROW_CENTRED + rnd + 1],
+                            in1=back[:].rearrange("q m b -> q (m b)"),
+                            op0=ALU.add,
+                            op1=ALU.subtract,
+                        )
+                    squares = tail.tile([P, BLOCKS, BATCH], F32)
+                    nc.scalar.activation(out=squares[:], in_=o[:, :, samples], func=ACT.Square)
+                    state["squares"] = squares
+
+                def scale():
+                    back = spread(
+                        group_sums(state["squares"][:], side), ACT.Abs_reciprocal_sqrt, eps[:, 0:1]
+                    )
+                    for j in range(BLOCKS):
+                        nc.vector.scalar_tensor_tensor(
+                            out=o[:, j, samples],
+                            in0=o[:, j, samples],
+                            scalar=cols[:, j, ROW_GAIN + side : ROW_GAIN + side + 1],
+                            in1=back[:].rearrange("q m b -> q (m b)"),
+                            op0=ALU.mult,
+                            op1=ALU.mult,
+                        )
+
+                def store():
+                    y = tail.tile([P, 2, ROUND_FIELDS, EMB], F32)
+                    for j0 in range(0, BLOCKS, 2):
+                        turned = aux_pool.tile([P, 2, 2, P], F32, tag="aux")
+                        nc.tensor.matmul(
+                            turned[:],
+                            lhsT=ident_bf[:, ROW_SHIFT + side : ROW_SHIFT + side + 1].to_broadcast(
+                                [P, P]
+                            ),
+                            rhs=shift_rows[:, j0 : j0 + 2, :].unsqueeze(2).to_broadcast([P, 2, 2, P]),
+                            start=True,
+                            stop=False,
+                        )
+                        for i in range(2):
+                            for m in range(2):
+                                first = side * BATCH + m * P
+                                nc.tensor.matmul(
+                                    turned[:, i, m, :],
+                                    lhsT=o[:, j0 + i, first : first + P],
+                                    rhs=ident[:],
+                                    is_transpose=True,
+                                    start=False,
+                                    stop=(i == 1 and m == 1),
+                                )
+                        nc.scalar.copy(
+                            out=y[:]
+                            .rearrange("b m g (j i) -> b j (m g) i", i=VALS)[:, j0 : j0 + 2],
+                            in_=turned[:].rearrange("b j m (g i) -> b j (m g) i", i=VALS),
+                        )
+                    nc.sync.dma_start(
+                        out=outs[side].rearrange("(m b) f d -> b m (f d)", m=2)[
+                            :, :, rnd * ROUND_COLS : (rnd + 1) * ROUND_COLS
+                        ],
+                        in_=y[:].rearrange("b m g d -> b m (g d)"),
+                    )
+
+                return centre, scale, store
+
+            weights = {step: prepare(step) for step in range(PREP_AHEAD)}
+            pending = []
+            o = None
+            for step in range(STEPS):
+                rnd, j = divmod(step, BLOCKS)
+                if step + PREP_AHEAD < STEPS:
+                    weights[step + PREP_AHEAD] = prepare(step + PREP_AHEAD)
+                if j == 0:
+                    o = tail.tile([P, BLOCKS, SAMPLES], F32, name="o")
+                codes, scales = weights.pop(step)
+                acc = acc_pool.tile([P, SAMPLES], F32)
+                for c in range(PASSES):
+                    nc.tensor.matmul_mx(
+                        out=acc[:],
+                        lhsT=codes[:, c, :].bitcast(FP8X4),
+                        lhsT_scale=scales[:, c, :],
+                        rhs=a_codes[:, c, :].bitcast(FP8X4),
+                        rhs_scale=a_scales[:, c, :],
+                        start=(c == 0),
+                        stop=(c == PASSES - 1),
+                    )
+                nc.vector.scalar_tensor_tensor(
+                    out=o[:, j, :],
+                    in0=acc[:],
+                    scalar=neg_bias[:, j, rnd : rnd + 1],
+                    in1=neg_polar[:, j, rnd, :],
+                    op0=ALU.max,
+                    op1=ALU.subtract,
+                )
+                if pending:
+                    pending.pop(0)()
+                if j == BLOCKS - 1:
+                    first, second = epilogue(rnd, 0, o), epilogue(rnd, 1, o)
+                    pending = [work for pair in zip(first, second) for work in pair]
+            for work in pending:
+                work()

@@ -32,7 +32,8 @@ STEPS = ROUNDS * BLOCKS
 THIRD = 2
 THIRDS = PASSES // THIRD
 LN_EPS = 1e-5
-PREP_AHEAD = 4
+PREP_AHEAD = 2
+HEAD_STEPS = 4
 ROUND_MAGIC = 12582912.0
 ROW_BIAS = 0
 ROW_CENTRED = 32
@@ -67,9 +68,10 @@ def tile_eulerinteractionlayer_pa_kernel(
     unpark = [x.rearrange("(j r q b) -> j q r b", j=BLOCKS, r=ROUNDS, q=P) for x in flat]
     with (
         tc.tile_pool(name="keep", bufs=1) as keep,
-        tc.tile_pool(name="w_raw", bufs=5) as w_raw_pool,
-        tc.tile_pool(name="w_grouped", bufs=3) as w_grouped_pool,
-        tc.tile_pool(name="w_mx", bufs=PREP_AHEAD + 2) as w_mx_pool,
+        tc.tile_pool(name="w_raw", bufs=2 * THIRDS - 1) as w_raw_pool,
+        tc.tile_pool(name="w_grouped", bufs=2) as w_grouped_pool,
+        tc.tile_pool(name="w_mx", bufs=PREP_AHEAD + 1) as w_mx_pool,
+        tc.tile_pool(name="o", bufs=2) as o_pool,
         tc.psum_pool(name="acc", bufs=3) as acc_pool,
         tc.psum_pool(name="aux", bufs=5) as aux_pool,
     ):
@@ -87,6 +89,7 @@ def tile_eulerinteractionlayer_pa_kernel(
         neg_bias = keep.tile([P, BLOCKS, ROUNDS], F32)
         shift_rows = keep.tile([P, BLOCKS, P], BF16)
         ident_bf = keep.tile([P, P], BF16)
+        mean_block = keep.tile([P, P], F32)
         polar_bias = keep.tile([P, 2, EMB], F32)
 
         w_raw = {}
@@ -109,7 +112,8 @@ def tile_eulerinteractionlayer_pa_kernel(
             for h in range(THIRDS):
                 if j == 0:
                     load_third(rnd, h)
-                regroup = nc.scalar.copy if (step * THIRDS + h) % 2 else nc.vector.tensor_copy
+                on_vector = step < HEAD_STEPS or (step * THIRDS + h) % 4 == 0
+                regroup = nc.vector.tensor_copy if on_vector else nc.scalar.copy
                 regroup(
                     out=grouped[:, h * THIRD : (h + 1) * THIRD, :, :].rearrange(
                         "q c (g i) t -> q c g t i", i=VALS
@@ -129,17 +133,10 @@ def tile_eulerinteractionlayer_pa_kernel(
             return codes, scales
 
         with tc.tile_pool(name="head", bufs=1) as head:
-            polar_rows = head.tile([P, P], BF16)
-            nc.gpsimd.memset(polar_rows[:], 0.0)
-            nc.sync.dma_start(out=polar_rows[0:EMB, :], in_=bias_theta.rearrange("o d g -> (o d) g"))
-            nc.sync.dma_start(
-                out=polar_rows[32 : 32 + EMB, :], in_=bias_lam.rearrange("o d g -> (o d) g")
-            )
-
             def load_rows(x):
                 tiles = []
                 for bt in range(2):
-                    raw = head.tile([P, K], BF16, tag="raw", bufs=4)
+                    raw = head.tile([P, K], BF16, tag="raw", bufs=3)
                     nc.sync.dma_start(
                         out=raw[:],
                         in_=x.rearrange("b f d -> b (f d)")[bt * P : (bt + 1) * P, :],
@@ -148,6 +145,13 @@ def tile_eulerinteractionlayer_pa_kernel(
                 return tiles
 
             raw_lam = load_rows(log_lam)
+            polar_rows = head.tile([P, P], BF16)
+            nc.gpsimd.memset(polar_rows[:], 0.0)
+            nc.sync.dma_start(out=polar_rows[0:EMB, :], in_=bias_theta.rearrange("o d g -> (o d) g"))
+            nc.sync.dma_start(
+                out=polar_rows[32 : 32 + EMB, :], in_=bias_lam.rearrange("o d g -> (o d) g")
+            )
+
             raw_theta = load_rows(theta)
             rows = head.tile([P, ROUND_FIELDS, EMB], BF16)
             nc.gpsimd.memset(rows[:], 0.0)
@@ -180,7 +184,33 @@ def tile_eulerinteractionlayer_pa_kernel(
             )
             nc.scalar.copy(out=polar_bias[:, 1, :], in_=flipped[:, 32 : 32 + EMB])
 
-            def mix(raws, finish):
+            raw_x = {}
+
+            def quantise_rows(side, c):
+                if c == 0:
+                    raw_x[side] = load_rows((r, p)[side])
+                samples = slice(side * BATCH, (side + 1) * BATCH)
+                grouped = head.tile([P, BATCH, 4], BF16, align_bytes=64, bufs=2)
+                flipped = aux_pool.tile([P, 2, 2, P], F32, tag="aux")
+                for i in range(2):
+                    words = raw_x[side][i][:].bitcast(F32)
+                    for u in range(2):
+                        nc.tensor.transpose(
+                            flipped[:, i, u, :],
+                            words[:, c * HALF + u : (c + 1) * HALF : 2],
+                            ident[:],
+                        )
+                nc.vector.tensor_copy(
+                    out=grouped[:].bitcast(F32).rearrange("q (i b) u -> q i b u", i=2),
+                    in_=flipped[:].rearrange("q i u b -> q i b u"),
+                )
+                nc.vector.quantize_mx(
+                    out=a_codes[:, c, samples].bitcast(FP8X4),
+                    scales=a_scales[:, c, samples],
+                    in_=grouped[:].rearrange("q n t -> q (n t)"),
+                )
+
+            def mix(raws, finish, finish_block):
                 for w0 in range(0, EMB // 2, 4):
                     x_t = head.tile([P, 4, BATCH, 2], BF16, bufs=2)
                     x_t_words = x_t[:].bitcast(F32)
@@ -209,6 +239,8 @@ def tile_eulerinteractionlayer_pa_kernel(
                         )
                         for e in range(2):
                             finish(2 * (w0 + i) + e, mixed[:, :, e])
+                        if i % 2:
+                            finish_block((w0 + i) // 2)
 
             held = neg_polar[:].rearrange("g j r s -> g j (r s)").rearrange(
                 "g j (t i b) -> g j t i b", t=2, i=VALS
@@ -231,9 +263,7 @@ def tile_eulerinteractionlayer_pa_kernel(
                     bias=polar_bias[:, 0, d : d + 1],
                 )
 
-            mix(raw_lam, finish_lam)
-            mix(raw_theta, finish_theta)
-            for j in range(BLOCKS):
+            def finish_polar(j):
                 lam = held[:, j, 0, :, :].rearrange("g i b -> g (i b)")
                 turns = held[:, j, 1, :, :].rearrange("g i b -> g (i b)")
                 part = head.tile([P, VALS * BATCH], F32, bufs=2)
@@ -258,38 +288,16 @@ def tile_eulerinteractionlayer_pa_kernel(
                 )
                 for side, term in ((0, part), (1, neg_sin)):
                     nc.sync.dma_start(out=park[side][j], in_=term[:])
-            for j in range(BLOCKS):
                 for side in range(SIDES):
                     nc.sync.dma_start(
                         out=neg_polar[:, j, :, side * BATCH : (side + 1) * BATCH],
                         in_=unpark[side][j],
                     )
+                for unit in (2 * j, 2 * j + 1):
+                    quantise_rows(*divmod(unit, PASSES))
 
-            raw_x = load_rows(r) + load_rows(p)
-            for c in range(PASSES):
-                grouped = head.tile([P, SAMPLES, 4], BF16, align_bytes=64, bufs=2)
-                grouped_words = grouped[:].bitcast(F32)
-                for m0 in range(0, M_TILES, 2):
-                    flipped = aux_pool.tile([P, 2, 2, P], F32, tag="aux")
-                    for i in range(2):
-                        words = raw_x[m0 + i][:].bitcast(F32)
-                        for u in range(2):
-                            nc.tensor.transpose(
-                                flipped[:, i, u, :],
-                                words[:, c * HALF + u : (c + 1) * HALF : 2],
-                                ident[:],
-                            )
-                    nc.vector.tensor_copy(
-                        out=grouped_words[:, m0 * P : (m0 + 2) * P, :].rearrange(
-                            "q (i b) u -> q i b u", i=2
-                        ),
-                        in_=flipped[:].rearrange("q i u b -> q i b u"),
-                    )
-                nc.vector.quantize_mx(
-                    out=a_codes[:, c, :].bitcast(FP8X4),
-                    scales=a_scales[:, c, :],
-                    in_=grouped[:].rearrange("q n t -> q (n t)"),
-                )
+            mix(raw_lam, finish_lam, lambda j: None)
+            mix(raw_theta, finish_theta, finish_polar)
 
             nc.vector.tensor_copy(
                 out=shift_rows[:].rearrange("k j (g i) -> k j g i", i=VALS),
@@ -314,6 +322,20 @@ def tile_eulerinteractionlayer_pa_kernel(
                 for i in range(3):
                     nc.tensor.transpose(flipped[:, i, :], rows_f32[:, j0 + i, :], ident[:])
                 nc.scalar.copy(out=cols[:, j0 : j0 + 3, :], in_=flipped[:, :, 0:68])
+            same_field = head.tile([P, ROUND_FIELDS], F32)
+            nc.vector.tensor_reduce(
+                out=same_field[:],
+                in_=ident[:].rearrange("q (g i) -> q g i", i=VALS),
+                axis=AXIS_X,
+                op=ALU.add,
+            )
+            nc.vector.tensor_scalar(
+                out=mean_block[:].rearrange("q (g i) -> q g i", i=VALS),
+                in0=same_field[:].unsqueeze(2).to_broadcast([P, ROUND_FIELDS, VALS]),
+                scalar1=1.0 / EMB,
+                scalar2=None,
+                op0=ALU.mult,
+            )
             nc.vector.tensor_scalar(
                 out=neg_bias[:],
                 in0=cols[:, :, ROW_BIAS : ROW_BIAS + ROUNDS],
@@ -324,20 +346,19 @@ def tile_eulerinteractionlayer_pa_kernel(
 
         with tc.tile_pool(name="tail", bufs=2) as tail:
 
-            def group_sums(x, side):
-                sums = aux_pool.tile([P, 2, P], F32, tag="aux")
-                for m in range(2):
-                    first = side * BATCH + m * P if x.shape[2] == SAMPLES else m * P
+            def group_sums(x, tiles):
+                sums = aux_pool.tile([P, tiles, P], F32, tag="aux", name="sums")
+                for m in range(tiles):
                     for j in range(BLOCKS):
                         nc.tensor.matmul(
                             sums[:, m, :],
-                            lhsT=x[:, j, first : first + P],
+                            lhsT=x[:, j, m * P : (m + 1) * P],
                             rhs=ident[:],
                             is_transpose=True,
                             start=(j == 0),
                             stop=(j == BLOCKS - 1),
                         )
-                total = tail.tile([P, 2 * ROUND_FIELDS], F32)
+                total = tail.tile([P, tiles * ROUND_FIELDS], F32, name="total")
                 nc.vector.tensor_reduce(
                     out=total[:],
                     in_=sums[:].rearrange("b m (g i) -> b (m g) i", i=VALS),
@@ -346,59 +367,115 @@ def tile_eulerinteractionlayer_pa_kernel(
                 )
                 return total
 
-            def spread(total, func, bias):
-                wide = tail.tile([P, 2 * ROUND_FIELDS, VALS], F32)
+            def spread(total, tiles, func, bias):
+                wide = tail.tile([P, tiles * ROUND_FIELDS, VALS], F32, name="wide")
                 nc.scalar.activation(
                     out=wide[:],
-                    in_=total[:].unsqueeze(2).to_broadcast([P, 2 * ROUND_FIELDS, VALS]),
+                    in_=total[:].unsqueeze(2).to_broadcast([P, tiles * ROUND_FIELDS, VALS]),
                     func=func,
                     scale=1.0 / EMB,
                     bias=bias,
                 )
-                back = aux_pool.tile([P, 2, P], F32, tag="aux")
-                for m in range(2):
+                return wide
+
+            def turn_back(wide, tiles):
+                back = aux_pool.tile([P, tiles, P], F32, tag="aux", name="back")
+                for m in range(tiles):
                     nc.tensor.transpose(
                         back[:, m, :],
-                        wide[:].rearrange("b (m g) i -> b m (g i)", m=2)[:, m, :],
+                        wide[:].rearrange("b (m g) i -> b m (g i)", m=tiles)[:, m, :],
                         ident[:],
                     )
-                return back
+                return back[:].rearrange("q m b -> q (m b)")
 
-            def epilogue(rnd, side, o):
-                samples = slice(side * BATCH, (side + 1) * BATCH)
+            def add_to_mean(mean, o, j):
+                nc.tensor.matmul(
+                    mean[:],
+                    lhsT=mean_block[:],
+                    rhs=o[:, j, :],
+                    start=(j == 0),
+                    stop=(j == BLOCKS - 1),
+                )
+
+            def epilogue(rnd, o, first_side, sides, known_mean=None):
+                tiles = 2 * sides
+                samples = slice(first_side * BATCH, (first_side + sides) * BATCH)
                 state = {}
 
+                def sum_values():
+                    state["wide"] = spread(group_sums(o[:, :, samples], tiles), tiles, ACT.Copy, 0.0)
+
                 def centre():
-                    back = spread(group_sums(o[:], side), ACT.Copy, 0.0)
+                    if known_mean is None:
+                        mean = turn_back(state["wide"], tiles)
+                    else:
+                        mean = known_mean[:, samples]
+                        sums = [acc_pool.tile([P, P], F32, name="acc") for m in range(tiles)]
+                    squares = tail.tile([P, BLOCKS, sides * BATCH], F32, name="squares", bufs=1)
                     for j in range(BLOCKS):
                         nc.vector.scalar_tensor_tensor(
                             out=o[:, j, samples],
                             in0=o[:, j, samples],
                             scalar=cols[:, j, ROW_CENTRED + rnd : ROW_CENTRED + rnd + 1],
-                            in1=back[:].rearrange("q m b -> q (m b)"),
+                            in1=mean,
                             op0=ALU.add,
                             op1=ALU.subtract,
                         )
-                    squares = tail.tile([P, BLOCKS, BATCH], F32)
-                    nc.scalar.activation(out=squares[:], in_=o[:, :, samples], func=ACT.Square)
+                        if j % 2:
+                            nc.scalar.activation(
+                                out=squares[:, j - 1 : j + 1, :],
+                                in_=o[:, j - 1 : j + 1, samples],
+                                func=ACT.Square,
+                            )
+                            if known_mean is not None:
+                                for i in (j - 1, j):
+                                    for m in range(tiles):
+                                        nc.tensor.matmul(
+                                            sums[m][:],
+                                            lhsT=squares[:, i, m * P : (m + 1) * P],
+                                            rhs=ident[:],
+                                            is_transpose=True,
+                                            start=(i == 0),
+                                            stop=(i == BLOCKS - 1),
+                                        )
+                    if known_mean is not None:
+                        total = tail.tile([P, tiles * ROUND_FIELDS], F32, name="total")
+                        for m in range(tiles):
+                            nc.vector.tensor_reduce(
+                                out=total[:, m * ROUND_FIELDS : (m + 1) * ROUND_FIELDS],
+                                in_=sums[m][:].rearrange("b (g i) -> b g i", i=VALS),
+                                axis=AXIS_X,
+                                op=ALU.add,
+                            )
+                        state["total"] = total
                     state["squares"] = squares
 
-                def scale():
-                    back = spread(
-                        group_sums(state["squares"][:], side), ACT.Abs_reciprocal_sqrt, eps[:, 0:1]
+                def sum_squares():
+                    if known_mean is None:
+                        state["total"] = group_sums(state["squares"][:], tiles)
+                    state["wide"] = spread(
+                        state["total"],
+                        tiles,
+                        ACT.Abs_reciprocal_sqrt,
+                        eps[:, 0:1],
                     )
-                    for j in range(BLOCKS):
-                        nc.vector.scalar_tensor_tensor(
-                            out=o[:, j, samples],
-                            in0=o[:, j, samples],
-                            scalar=cols[:, j, ROW_GAIN + side : ROW_GAIN + side + 1],
-                            in1=back[:].rearrange("q m b -> q (m b)"),
-                            op0=ALU.mult,
-                            op1=ALU.mult,
-                        )
 
-                def store():
-                    y = tail.tile([P, 2, ROUND_FIELDS, EMB], F32)
+                def scale():
+                    rstd = turn_back(state["wide"], tiles)
+                    for side in range(first_side, first_side + sides):
+                        for j in range(BLOCKS):
+                            first = (side - first_side) * BATCH
+                            nc.vector.scalar_tensor_tensor(
+                                out=o[:, j, side * BATCH : (side + 1) * BATCH],
+                                in0=o[:, j, side * BATCH : (side + 1) * BATCH],
+                                scalar=cols[:, j, ROW_GAIN + side : ROW_GAIN + side + 1],
+                                in1=rstd[:, first : first + BATCH],
+                                op0=ALU.mult,
+                                op1=ALU.mult,
+                            )
+
+                def store(side):
+                    y = tail.tile([P, 2, ROUND_FIELDS, EMB], F32, name="y")
                     for j0 in range(0, BLOCKS, 2):
                         turned = aux_pool.tile([P, 2, 2, P], F32, tag="aux")
                         nc.tensor.matmul(
@@ -433,19 +510,14 @@ def tile_eulerinteractionlayer_pa_kernel(
                         in_=y[:].rearrange("b m g d -> b m (g d)"),
                     )
 
-                return centre, scale, store
+                stores = [lambda side=side: store(side) for side in range(first_side, first_side + sides)]
+                if known_mean is None:
+                    return [sum_values, centre, sum_squares, scale] + stores
+                return [centre, sum_squares, scale] + stores
 
-            weights = {step: prepare(step) for step in range(PREP_AHEAD)}
-            pending = []
-            o = None
-            for step in range(STEPS):
-                rnd, j = divmod(step, BLOCKS)
-                if step + PREP_AHEAD < STEPS:
-                    weights[step + PREP_AHEAD] = prepare(step + PREP_AHEAD)
-                if j == 0:
-                    o = tail.tile([P, BLOCKS, SAMPLES], F32, name="o")
-                codes, scales = weights.pop(step)
-                acc = acc_pool.tile([P, SAMPLES], F32)
+            def multiply(step):
+                codes, scales = weights[step]
+                acc = acc_pool.tile([P, SAMPLES], F32, name="acc")
                 for c in range(PASSES):
                     nc.tensor.matmul_mx(
                         out=acc[:],
@@ -456,6 +528,10 @@ def tile_eulerinteractionlayer_pa_kernel(
                         start=(c == 0),
                         stop=(c == PASSES - 1),
                     )
+                return acc
+
+            def combine(step, acc, o):
+                rnd, j = divmod(step, BLOCKS)
                 nc.vector.scalar_tensor_tensor(
                     out=o[:, j, :],
                     in0=acc[:],
@@ -464,10 +540,36 @@ def tile_eulerinteractionlayer_pa_kernel(
                     op0=ALU.max,
                     op1=ALU.subtract,
                 )
+
+            weights = {step: prepare(step) for step in range(PREP_AHEAD)}
+            pending = []
+            o = None
+            mean = None
+            acc = multiply(0)
+            for step in range(STEPS):
+                rnd, j = divmod(step, BLOCKS)
+                if j == 0:
+                    o = o_pool.tile([P, BLOCKS, SAMPLES], F32, name="o")
+                next_acc = multiply(step + 1) if step + 1 < STEPS else None
+                combine(step, acc, o)
+                acc = next_acc
                 if pending:
                     pending.pop(0)()
+                if rnd == ROUNDS - 1:
+                    if j == 0:
+                        mean = aux_pool.tile([P, SAMPLES], F32, tag="aux", name="mean")
+                    add_to_mean(mean, o, j)
+                if step + PREP_AHEAD < STEPS:
+                    weights[step + PREP_AHEAD] = prepare(step + PREP_AHEAD)
                 if j == BLOCKS - 1:
-                    first, second = epilogue(rnd, 0, o), epilogue(rnd, 1, o)
-                    pending = [work for pair in zip(first, second) for work in pair]
+                    pending = epilogue(rnd, o, 0, SIDES)
+                    if rnd == ROUNDS - 1:
+                        pending = [
+                            work
+                            for pair in zip(
+                                epilogue(rnd, o, 0, 1, mean), epilogue(rnd, o, 1, 1, mean)
+                            )
+                            for work in pair
+                        ]
             for work in pending:
                 work()

@@ -5,6 +5,7 @@ from concourse.masks import make_identity
 
 F32 = mybir.dt.float32
 BF16 = mybir.dt.bfloat16
+I32 = mybir.dt.int32
 U32 = mybir.dt.uint32
 U8 = mybir.dt.uint8
 FP8X4 = mybir.dt.float8_e4m3fn_x4
@@ -33,8 +34,7 @@ THIRD = 2
 THIRDS = PASSES // THIRD
 LN_EPS = 1e-5
 PREP_AHEAD = 2
-HEAD_STEPS = 4
-ROUND_MAGIC = 12582912.0
+HEAD_STEPS = 2
 ROW_BIAS = 0
 ROW_CENTRED = 32
 ROW_GAIN = 64
@@ -68,10 +68,10 @@ def tile_eulerinteractionlayer_pa_kernel(
     unpark = [x.rearrange("(j r q b) -> j q r b", j=BLOCKS, r=ROUNDS, q=P) for x in flat]
     with (
         tc.tile_pool(name="keep", bufs=1) as keep,
-        tc.tile_pool(name="w_raw", bufs=2 * THIRDS - 1) as w_raw_pool,
+        tc.tile_pool(name="w_raw", bufs=2 * THIRDS) as w_raw_pool,
         tc.tile_pool(name="w_grouped", bufs=2) as w_grouped_pool,
         tc.tile_pool(name="w_mx", bufs=PREP_AHEAD + 1) as w_mx_pool,
-        tc.tile_pool(name="o", bufs=2) as o_pool,
+        tc.tile_pool(name="o", bufs=1) as o_pool,
         tc.psum_pool(name="acc", bufs=3) as acc_pool,
         tc.psum_pool(name="aux", bufs=5) as aux_pool,
     ):
@@ -87,10 +87,10 @@ def tile_eulerinteractionlayer_pa_kernel(
         neg_polar = keep.tile([P, BLOCKS, ROUNDS, SAMPLES], F32)
         cols = keep.tile([P, BLOCKS, 68], F32)
         neg_bias = keep.tile([P, BLOCKS, ROUNDS], F32)
-        shift_rows = keep.tile([P, BLOCKS, P], BF16)
         ident_bf = keep.tile([P, P], BF16)
+        shift_rows = keep.tile([P, BLOCKS, P], BF16)
+        lam_bias = keep.tile([P, EMB], F32)
         mean_block = keep.tile([P, P], F32)
-        polar_bias = keep.tile([P, 2, EMB], F32)
 
         w_raw = {}
 
@@ -172,17 +172,12 @@ def tile_eulerinteractionlayer_pa_kernel(
                 )
 
             nc.vector.tensor_copy(out=ident_bf[:], in_=ident[:])
-            polar_rows_f32 = head.tile([P, P], F32)
-            nc.vector.tensor_copy(out=polar_rows_f32[:], in_=polar_rows[:])
+
+            lam_rows = head.tile([P, P], F32)
+            nc.vector.tensor_copy(out=lam_rows[:], in_=polar_rows[:])
             flipped = aux_pool.tile([P, P], F32, tag="aux")
-            nc.tensor.transpose(flipped[:], polar_rows_f32[:], ident[:])
-            nc.scalar.activation(
-                out=polar_bias[:, 0, :],
-                in_=flipped[:, 0:EMB],
-                func=ACT.Copy,
-                scale=1.0 / (2.0 * math.pi),
-            )
-            nc.scalar.copy(out=polar_bias[:, 1, :], in_=flipped[:, 32 : 32 + EMB])
+            nc.tensor.transpose(flipped[:], lam_rows[:], ident[:])
+            nc.scalar.copy(out=lam_bias[:], in_=flipped[:, 32 : 32 + EMB])
 
             raw_x = {}
 
@@ -210,16 +205,17 @@ def tile_eulerinteractionlayer_pa_kernel(
                     in_=grouped[:].rearrange("q n t -> q (n t)"),
                 )
 
-            def mix(raws, finish, finish_block):
+            def turn(raws):
+                tiles = []
                 for w0 in range(0, EMB // 2, 4):
-                    x_t = head.tile([P, 4, BATCH, 2], BF16, bufs=2)
+                    x_t = head.tile([P, 4, BATCH, 2], BF16, bufs=3)
                     x_t_words = x_t[:].bitcast(F32)
                     for bt in range(2):
                         by_word = head.tile([P, 4, FIELDS], F32, bufs=2)
                         nc.vector.tensor_copy(
-                            out=by_word[:],
-                            in_=raws[bt][:].bitcast(F32).rearrange("b (f w) -> b w f", w=EMB // 2)[
-                                :, w0 : w0 + 4, :
+                            out=by_word[:].rearrange("b w f -> b f w"),
+                            in_=raws[bt][:].bitcast(F32).rearrange("b (f w) -> b f w", w=EMB // 2)[
+                                :, :, w0 : w0 + 4
                             ],
                         )
                         flipped = aux_pool.tile([P, 4, P], F32, tag="aux")
@@ -228,66 +224,84 @@ def tile_eulerinteractionlayer_pa_kernel(
                         nc.scalar.copy(
                             out=x_t_words[:, :, bt * P : (bt + 1) * P, 0], in_=flipped[:]
                         )
+                    tiles.append(x_t)
+                return tiles
+
+            def mix(tiles, add_bias, finish, finish_block):
+                for w0, x_t in zip(range(0, EMB // 2, 4), tiles):
                     for i in range(4):
                         mixed = aux_pool.tile([P, BATCH, 2], F32, tag="aux")
+                        if add_bias:
+                            row = 2 * (w0 + i)
+                            nc.tensor.matmul(
+                                mixed[:],
+                                lhsT=polar_rows[:],
+                                rhs=ident_bf[:, row : row + 2]
+                                .unsqueeze(1)
+                                .to_broadcast([P, BATCH, 2]),
+                                start=True,
+                                stop=False,
+                            )
                         nc.tensor.matmul(
                             mixed[:].rearrange("g b e -> g (b e)"),
                             lhsT=orders[:],
                             rhs=x_t[:, i, :, :].rearrange("f b e -> f (b e)"),
-                            start=True,
+                            start=not add_bias,
                             stop=True,
                         )
-                        for e in range(2):
-                            finish(2 * (w0 + i) + e, mixed[:, :, e])
+                        finish(2 * (w0 + i), mixed[:].rearrange("g b e -> g e b"))
                         if i % 2:
                             finish_block((w0 + i) // 2)
 
             held = neg_polar[:].rearrange("g j r s -> g j (r s)").rearrange(
                 "g j (t i b) -> g j t i b", t=2, i=VALS
             )
+            angles = {}
 
             def finish_lam(d, mixed):
-                nc.scalar.activation(
-                    out=held[:, d // VALS, 0, d % VALS, :],
-                    in_=mixed,
-                    func=ACT.Exp,
-                    bias=polar_bias[:, 1, d : d + 1],
-                )
+                j, i = divmod(d, VALS)
+                for e in range(2):
+                    nc.scalar.activation(
+                        out=held[:, j, 0, i + e, :],
+                        in_=mixed[:, e, :],
+                        func=ACT.Exp,
+                        bias=lam_bias[:, d + e : d + e + 1],
+                    )
 
             def finish_theta(d, mixed):
-                nc.scalar.activation(
-                    out=held[:, d // VALS, 1, d % VALS, :],
-                    in_=mixed,
-                    func=ACT.Identity,
-                    scale=1.0 / (2.0 * math.pi),
-                    bias=polar_bias[:, 0, d : d + 1],
+                j, i = divmod(d, VALS)
+                if i == 0:
+                    angles[j] = head.tile([P, VALS, BATCH], F32, name="angle", bufs=2)
+                turns = head.tile([P, 2, BATCH], I32)
+                nc.vector.tensor_scalar(
+                    out=turns[:],
+                    in0=mixed,
+                    scalar1=1.0 / (2.0 * math.pi),
+                    scalar2=None,
+                    op0=ALU.mult,
+                )
+                nc.vector.scalar_tensor_tensor(
+                    out=angles[j][:, i : i + 2, :],
+                    in0=mixed,
+                    scalar=1.0 / (2.0 * math.pi),
+                    in1=turns[:],
+                    op0=ALU.mult,
+                    op1=ALU.subtract,
                 )
 
             def finish_polar(j):
                 lam = held[:, j, 0, :, :].rearrange("g i b -> g (i b)")
-                turns = held[:, j, 1, :, :].rearrange("g i b -> g (i b)")
-                part = head.tile([P, VALS * BATCH], F32, bufs=2)
-                nc.vector.tensor_scalar(
-                    out=part[:],
-                    in0=turns,
-                    scalar1=ROUND_MAGIC,
-                    scalar2=ROUND_MAGIC,
-                    op0=ALU.add,
-                    op1=ALU.subtract,
-                )
-                nc.vector.tensor_tensor(out=part[:], in0=part[:], in1=turns, op=ALU.subtract)
+                angle = angles.pop(j)[:].rearrange("g i b -> g (i b)")
                 neg_sin = head.tile([P, VALS * BATCH], F32, bufs=2)
-                nc.scalar.activation(out=neg_sin[:], in_=part[:], func=ACT.Sin, scale=2.0 * math.pi)
-                nc.scalar.activation(out=part[:], in_=part[:], func=ACT.Sin, scale=math.pi)
-                nc.scalar.activation(
-                    out=part[:], in_=part[:], func=ACT.Square, scale=math.sqrt(2.0)
-                )
+                nc.scalar.activation(out=neg_sin[:], in_=angle, func=ACT.Sin, scale=-2.0 * math.pi)
+                nc.scalar.activation(out=angle, in_=angle, func=ACT.Sin, scale=math.pi)
+                nc.scalar.activation(out=angle, in_=angle, func=ACT.Square, scale=math.sqrt(2.0))
                 nc.vector.tensor_tensor(out=neg_sin[:], in0=neg_sin[:], in1=lam, op=ALU.mult)
                 nc.vector.scalar_tensor_tensor(
-                    out=part[:], in0=part[:], scalar=1.0, in1=lam, op0=ALU.subtract, op1=ALU.mult
+                    out=angle, in0=angle, scalar=1.0, in1=lam, op0=ALU.subtract, op1=ALU.mult
                 )
-                for side, term in ((0, part), (1, neg_sin)):
-                    nc.sync.dma_start(out=park[side][j], in_=term[:])
+                for side, term in ((0, angle), (1, neg_sin[:])):
+                    nc.sync.dma_start(out=park[side][j], in_=term)
                 for side in range(SIDES):
                     nc.sync.dma_start(
                         out=neg_polar[:, j, :, side * BATCH : (side + 1) * BATCH],
@@ -296,8 +310,8 @@ def tile_eulerinteractionlayer_pa_kernel(
                 for unit in (2 * j, 2 * j + 1):
                     quantise_rows(*divmod(unit, PASSES))
 
-            mix(raw_lam, finish_lam, lambda j: None)
-            mix(raw_theta, finish_theta, finish_polar)
+            mix(turn(raw_lam), False, finish_lam, lambda j: None)
+            mix(turn(raw_theta), True, finish_theta, finish_polar)
 
             nc.vector.tensor_copy(
                 out=shift_rows[:].rearrange("k j (g i) -> k j g i", i=VALS),
@@ -478,16 +492,20 @@ def tile_eulerinteractionlayer_pa_kernel(
                     y = tail.tile([P, 2, ROUND_FIELDS, EMB], F32, name="y")
                     for j0 in range(0, BLOCKS, 2):
                         turned = aux_pool.tile([P, 2, 2, P], F32, tag="aux")
-                        nc.tensor.matmul(
-                            turned[:],
-                            lhsT=ident_bf[:, ROW_SHIFT + side : ROW_SHIFT + side + 1].to_broadcast(
-                                [P, P]
-                            ),
-                            rhs=shift_rows[:, j0 : j0 + 2, :].unsqueeze(2).to_broadcast([P, 2, 2, P]),
-                            start=True,
-                            stop=False,
-                        )
+                        by_product = rnd < 2
+                        if by_product:
+                            row = ROW_SHIFT + side
+                            nc.tensor.matmul(
+                                turned[:],
+                                lhsT=ident_bf[:, row : row + 1].to_broadcast([P, P]),
+                                rhs=shift_rows[:, j0 : j0 + 2, :]
+                                .unsqueeze(2)
+                                .to_broadcast([P, 2, 2, P]),
+                                start=True,
+                                stop=False,
+                            )
                         for i in range(2):
+                            shift = cols[:, j0 + i, ROW_SHIFT + side : ROW_SHIFT + side + 1]
                             for m in range(2):
                                 first = side * BATCH + m * P
                                 nc.tensor.matmul(
@@ -495,9 +513,18 @@ def tile_eulerinteractionlayer_pa_kernel(
                                     lhsT=o[:, j0 + i, first : first + P],
                                     rhs=ident[:],
                                     is_transpose=True,
-                                    start=False,
-                                    stop=(i == 1 and m == 1),
+                                    start=not by_product,
+                                    stop=by_product and i == 1 and m == 1,
                                 )
+                                if not by_product:
+                                    nc.tensor.matmul(
+                                        turned[:, i, m, :],
+                                        lhsT=shift.to_broadcast([P, P]),
+                                        rhs=ident[:],
+                                        is_transpose=True,
+                                        start=False,
+                                        stop=True,
+                                    )
                         nc.scalar.copy(
                             out=y[:]
                             .rearrange("b m g (j i) -> b j (m g) i", i=VALS)[:, j0 : j0 + 2],
@@ -549,7 +576,9 @@ def tile_eulerinteractionlayer_pa_kernel(
             for step in range(STEPS):
                 rnd, j = divmod(step, BLOCKS)
                 if j == 0:
-                    o = o_pool.tile([P, BLOCKS, SAMPLES], F32, name="o")
+                    o = (tail if rnd % 2 else o_pool).tile(
+                        [P, BLOCKS, SAMPLES], F32, name="o", bufs=1
+                    )
                 next_acc = multiply(step + 1) if step + 1 < STEPS else None
                 combine(step, acc, o)
                 acc = next_acc

@@ -33,8 +33,9 @@ STEPS = ROUNDS * BLOCKS
 THIRD = 2
 THIRDS = PASSES // THIRD
 LN_EPS = 1e-5
+HEAD_ADVANCE = 3
 PREP_AHEAD = 2
-HEAD_STEPS = 2
+HEAD_STEPS = 1
 ROW_BIAS = 0
 ROW_CENTRED = 32
 ROW_GAIN = 64
@@ -112,7 +113,7 @@ def tile_eulerinteractionlayer_pa_kernel(
             for h in range(THIRDS):
                 if j == 0:
                     load_third(rnd, h)
-                on_vector = step < HEAD_STEPS or (step * THIRDS + h) % 4 == 0
+                on_vector = step < HEAD_STEPS or (step * THIRDS + h) % 3 == 0
                 regroup = nc.vector.tensor_copy if on_vector else nc.scalar.copy
                 regroup(
                     out=grouped[:, h * THIRD : (h + 1) * THIRD, :, :].rearrange(
@@ -131,6 +132,44 @@ def tile_eulerinteractionlayer_pa_kernel(
                     in_=grouped[:, lo:hi, :, :].rearrange("q c n t -> q (c n t)"),
                 )
             return codes, scales
+
+        def multiply(step):
+            codes, scales = weights[step]
+            acc = acc_pool.tile([P, SAMPLES], F32, name="acc")
+            for c in range(PASSES):
+                nc.tensor.matmul_mx(
+                    out=acc[:],
+                    lhsT=codes[:, c, :].bitcast(FP8X4),
+                    lhsT_scale=scales[:, c, :],
+                    rhs=a_codes[:, c, :].bitcast(FP8X4),
+                    rhs_scale=a_scales[:, c, :],
+                    start=(c == 0),
+                    stop=(c == PASSES - 1),
+                )
+            return acc
+
+        def combine(step, acc, o):
+            rnd, j = divmod(step, BLOCKS)
+            nc.vector.scalar_tensor_tensor(
+                out=o[:, j, :],
+                in0=acc[:],
+                scalar=neg_bias[:, j, rnd : rnd + 1],
+                in1=neg_polar[:, j, rnd, :],
+                op0=ALU.max,
+                op1=ALU.subtract,
+            )
+
+        weights = {}
+        products = {}
+
+        def advance(step, o):
+            if step + 1 < STEPS:
+                products[step + 1] = multiply(step + 1)
+            combine(step, products.pop(step), o)
+            if step + PREP_AHEAD < STEPS:
+                weights[step + PREP_AHEAD] = prepare(step + PREP_AHEAD)
+
+        first_o = o_pool.tile([P, BLOCKS, SAMPLES], F32, name="o")
 
         with tc.tile_pool(name="head", bufs=1) as head:
             def load_rows(x):
@@ -181,29 +220,33 @@ def tile_eulerinteractionlayer_pa_kernel(
 
             raw_x = {}
 
-            def quantise_rows(side, c):
-                if c == 0:
+            def quantise_rows(side, c0):
+                if c0 == 0:
                     raw_x[side] = load_rows((r, p)[side])
                 samples = slice(side * BATCH, (side + 1) * BATCH)
-                grouped = head.tile([P, BATCH, 4], BF16, align_bytes=64, bufs=2)
-                flipped = aux_pool.tile([P, 2, 2, P], F32, tag="aux")
-                for i in range(2):
-                    words = raw_x[side][i][:].bitcast(F32)
-                    for u in range(2):
-                        nc.tensor.transpose(
-                            flipped[:, i, u, :],
-                            words[:, c * HALF + u : (c + 1) * HALF : 2],
-                            ident[:],
-                        )
-                nc.vector.tensor_copy(
-                    out=grouped[:].bitcast(F32).rearrange("q (i b) u -> q i b u", i=2),
-                    in_=flipped[:].rearrange("q i u b -> q i b u"),
-                )
-                nc.vector.quantize_mx(
-                    out=a_codes[:, c, samples].bitcast(FP8X4),
-                    scales=a_scales[:, c, samples],
-                    in_=grouped[:].rearrange("q n t -> q (n t)"),
-                )
+                tiles = []
+                for c in (c0, c0 + 1):
+                    grouped = head.tile([P, BATCH, 4], BF16, align_bytes=64, bufs=2)
+                    flipped = aux_pool.tile([P, 2, 2, P], F32, tag="aux")
+                    for i in range(2):
+                        words = raw_x[side][i][:].bitcast(F32)
+                        for u in range(2):
+                            nc.tensor.transpose(
+                                flipped[:, i, u, :],
+                                words[:, c * HALF + u : (c + 1) * HALF : 2],
+                                ident[:],
+                            )
+                    nc.scalar.copy(
+                        out=grouped[:].bitcast(F32).rearrange("q (i b) u -> q i b u", i=2),
+                        in_=flipped[:].rearrange("q i u b -> q i b u"),
+                    )
+                    tiles.append(grouped)
+                for c, grouped in zip((c0, c0 + 1), tiles):
+                    nc.vector.quantize_mx(
+                        out=a_codes[:, c, samples].bitcast(FP8X4),
+                        scales=a_scales[:, c, samples],
+                        in_=grouped[:].rearrange("q n t -> q (n t)"),
+                    )
 
             def turn(raws):
                 tiles = []
@@ -227,7 +270,8 @@ def tile_eulerinteractionlayer_pa_kernel(
                     tiles.append(x_t)
                 return tiles
 
-            def mix(tiles, add_bias, finish, finish_block):
+            def mix(tiles, add_bias, finish):
+                pair = []
                 for w0, x_t in zip(range(0, EMB // 2, 4), tiles):
                     for i in range(4):
                         mixed = aux_pool.tile([P, BATCH, 2], F32, tag="aux")
@@ -249,49 +293,48 @@ def tile_eulerinteractionlayer_pa_kernel(
                             start=not add_bias,
                             stop=True,
                         )
-                        finish(2 * (w0 + i), mixed[:].rearrange("g b e -> g e b"))
+                        pair.append(mixed[:].rearrange("g b e -> g e b"))
                         if i % 2:
-                            finish_block((w0 + i) // 2)
+                            finish((w0 + i) // 2, pair)
+                            pair = []
 
             held = neg_polar[:].rearrange("g j r s -> g j (r s)").rearrange(
                 "g j (t i b) -> g j t i b", t=2, i=VALS
             )
-            angles = {}
 
-            def finish_lam(d, mixed):
-                j, i = divmod(d, VALS)
-                for e in range(2):
+            def finish_lam(j, pair):
+                for i in range(VALS):
                     nc.scalar.activation(
-                        out=held[:, j, 0, i + e, :],
-                        in_=mixed[:, e, :],
+                        out=held[:, j, 0, i, :],
+                        in_=pair[i // 2][:, i % 2, :],
                         func=ACT.Exp,
-                        bias=lam_bias[:, d + e : d + e + 1],
+                        bias=lam_bias[:, j * VALS + i : j * VALS + i + 1],
                     )
 
-            def finish_theta(d, mixed):
-                j, i = divmod(d, VALS)
-                if i == 0:
-                    angles[j] = head.tile([P, VALS, BATCH], F32, name="angle", bufs=2)
-                turns = head.tile([P, 2, BATCH], I32)
-                nc.vector.tensor_scalar(
-                    out=turns[:],
-                    in0=mixed,
-                    scalar1=1.0 / (2.0 * math.pi),
-                    scalar2=None,
-                    op0=ALU.mult,
-                )
-                nc.vector.scalar_tensor_tensor(
-                    out=angles[j][:, i : i + 2, :],
-                    in0=mixed,
-                    scalar=1.0 / (2.0 * math.pi),
-                    in1=turns[:],
-                    op0=ALU.mult,
-                    op1=ALU.subtract,
-                )
-
-            def finish_polar(j):
+            def finish_theta(j, pair):
+                block_angle = head.tile([P, VALS, BATCH], F32, name="angle", bufs=2)
+                turns = []
+                for mixed in pair:
+                    whole = head.tile([P, 2, BATCH], I32, name="whole", bufs=2)
+                    nc.vector.tensor_scalar(
+                        out=whole[:],
+                        in0=mixed,
+                        scalar1=1.0 / (2.0 * math.pi),
+                        scalar2=None,
+                        op0=ALU.mult,
+                    )
+                    turns.append(whole)
+                for i, mixed in enumerate(pair):
+                    nc.vector.scalar_tensor_tensor(
+                        out=block_angle[:, 2 * i : 2 * i + 2, :],
+                        in0=mixed,
+                        scalar=1.0 / (2.0 * math.pi),
+                        in1=turns[i][:],
+                        op0=ALU.mult,
+                        op1=ALU.subtract,
+                    )
+                angle = block_angle[:].rearrange("g i b -> g (i b)")
                 lam = held[:, j, 0, :, :].rearrange("g i b -> g (i b)")
-                angle = angles.pop(j)[:].rearrange("g i b -> g (i b)")
                 neg_sin = head.tile([P, VALS * BATCH], F32, bufs=2)
                 nc.scalar.activation(out=neg_sin[:], in_=angle, func=ACT.Sin, scale=-2.0 * math.pi)
                 nc.scalar.activation(out=angle, in_=angle, func=ACT.Sin, scale=math.pi)
@@ -307,11 +350,17 @@ def tile_eulerinteractionlayer_pa_kernel(
                         out=neg_polar[:, j, :, side * BATCH : (side + 1) * BATCH],
                         in_=unpark[side][j],
                     )
-                for unit in (2 * j, 2 * j + 1):
-                    quantise_rows(*divmod(unit, PASSES))
+                if j < 3:
+                    for unit in (4 * j, 4 * j + 2):
+                        quantise_rows(*divmod(unit, PASSES))
+                if j == 2:
+                    for step in range(PREP_AHEAD):
+                        weights[step] = prepare(step)
+                    products[0] = multiply(0)
+                if j > 2:
+                    advance(j - 3, first_o)
 
-            mix(turn(raw_lam), False, finish_lam, lambda j: None)
-            mix(turn(raw_theta), True, finish_theta, finish_polar)
+            mix(turn(raw_lam), False, finish_lam)
 
             nc.vector.tensor_copy(
                 out=shift_rows[:].rearrange("k j (g i) -> k j g i", i=VALS),
@@ -357,6 +406,9 @@ def tile_eulerinteractionlayer_pa_kernel(
                 scalar2=None,
                 op0=ALU.mult,
             )
+
+            mix(turn(raw_theta), True, finish_theta)
+
 
         with tc.tile_pool(name="tail", bufs=2) as tail:
 
@@ -492,7 +544,7 @@ def tile_eulerinteractionlayer_pa_kernel(
                     y = tail.tile([P, 2, ROUND_FIELDS, EMB], F32, name="y")
                     for j0 in range(0, BLOCKS, 2):
                         turned = aux_pool.tile([P, 2, 2, P], F32, tag="aux")
-                        by_product = rnd < 2
+                        by_product = rnd >= 2
                         if by_product:
                             row = ROW_SHIFT + side
                             nc.tensor.matmul(
@@ -525,7 +577,8 @@ def tile_eulerinteractionlayer_pa_kernel(
                                         start=False,
                                         stop=True,
                                     )
-                        nc.scalar.copy(
+                        copy = nc.vector.tensor_copy if known_mean is not None and j0 == 2 else nc.scalar.copy
+                        copy(
                             out=y[:]
                             .rearrange("b m g (j i) -> b j (m g) i", i=VALS)[:, j0 : j0 + 2],
                             in_=turned[:].rearrange("b j m (g i) -> b j (m g) i", i=VALS),
@@ -542,57 +595,25 @@ def tile_eulerinteractionlayer_pa_kernel(
                     return [sum_values, centre, sum_squares, scale] + stores
                 return [centre, sum_squares, scale] + stores
 
-            def multiply(step):
-                codes, scales = weights[step]
-                acc = acc_pool.tile([P, SAMPLES], F32, name="acc")
-                for c in range(PASSES):
-                    nc.tensor.matmul_mx(
-                        out=acc[:],
-                        lhsT=codes[:, c, :].bitcast(FP8X4),
-                        lhsT_scale=scales[:, c, :],
-                        rhs=a_codes[:, c, :].bitcast(FP8X4),
-                        rhs_scale=a_scales[:, c, :],
-                        start=(c == 0),
-                        stop=(c == PASSES - 1),
-                    )
-                return acc
-
-            def combine(step, acc, o):
-                rnd, j = divmod(step, BLOCKS)
-                nc.vector.scalar_tensor_tensor(
-                    out=o[:, j, :],
-                    in0=acc[:],
-                    scalar=neg_bias[:, j, rnd : rnd + 1],
-                    in1=neg_polar[:, j, rnd, :],
-                    op0=ALU.max,
-                    op1=ALU.subtract,
-                )
-
-            weights = {step: prepare(step) for step in range(PREP_AHEAD)}
             pending = []
-            o = None
+            o = first_o
             mean = None
-            acc = multiply(0)
-            for step in range(STEPS):
+            for step in range(HEAD_ADVANCE, STEPS):
                 rnd, j = divmod(step, BLOCKS)
                 if j == 0:
-                    o = (tail if rnd % 2 else o_pool).tile(
-                        [P, BLOCKS, SAMPLES], F32, name="o", bufs=1
-                    )
-                next_acc = multiply(step + 1) if step + 1 < STEPS else None
-                combine(step, acc, o)
-                acc = next_acc
-                if pending:
-                    pending.pop(0)()
+                    o = (tail if rnd % 2 else o_pool).tile([P, BLOCKS, SAMPLES], F32, name="o", bufs=1)
                 if rnd == ROUNDS - 1:
                     if j == 0:
                         mean = aux_pool.tile([P, SAMPLES], F32, tag="aux", name="mean")
-                    add_to_mean(mean, o, j)
-                if step + PREP_AHEAD < STEPS:
-                    weights[step + PREP_AHEAD] = prepare(step + PREP_AHEAD)
+                    else:
+                        add_to_mean(mean, o, j - 1)
+                if pending:
+                    pending.pop(0)()
+                advance(step, o)
                 if j == BLOCKS - 1:
                     pending = epilogue(rnd, o, 0, SIDES)
                     if rnd == ROUNDS - 1:
+                        add_to_mean(mean, o, j)
                         pending = [
                             work
                             for pair in zip(

@@ -96,7 +96,7 @@ def tile_eulerinteractionlayer_pa_kernel(
         w_raw = {}
 
         def load_third(rnd, h):
-            tile = w_raw_pool.tile([P, THIRD, 4, ROUND_COLS], BF16, name="w_third")
+            tile = w_raw_pool.tile([P, THIRD, 4, ROUND_COLS], BF16, name="w_third", tag="w_raw")
             for i in range(THIRD):
                 first = (h * THIRD + i) * K_PASS
                 nc.sync.dma_start(
@@ -111,7 +111,7 @@ def tile_eulerinteractionlayer_pa_kernel(
             rnd, j = divmod(step, BLOCKS)
             grouped = w_grouped_pool.tile([P, PASSES, P, 4], BF16, align_bytes=64)
             for h in range(THIRDS):
-                if j == 0:
+                if j == 0 and rnd:
                     load_third(rnd, h)
                 on_vector = step < HEAD_STEPS or (step * THIRDS + h) % 3 == 0
                 regroup = nc.vector.tensor_copy if on_vector else nc.scalar.copy
@@ -133,9 +133,10 @@ def tile_eulerinteractionlayer_pa_kernel(
                 )
             return codes, scales
 
-        def multiply(step):
+        def multiply(step, jobs):
             codes, scales = weights[step]
             acc = acc_pool.tile([P, SAMPLES], F32, name="acc")
+            slots = PASSES // 2
             for c in range(PASSES):
                 nc.tensor.matmul_mx(
                     out=acc[:],
@@ -146,6 +147,10 @@ def tile_eulerinteractionlayer_pa_kernel(
                     start=(c == 0),
                     stop=(c == PASSES - 1),
                 )
+                if c % 2:
+                    slot = c // 2
+                    for job in jobs[slot * len(jobs) // slots : (slot + 1) * len(jobs) // slots]:
+                        job()
             return acc
 
         def combine(step, acc, o):
@@ -162,10 +167,15 @@ def tile_eulerinteractionlayer_pa_kernel(
         weights = {}
         products = {}
 
-        def advance(step, o):
+        def advance(step, o, jobs=(), rest=None):
             if step + 1 < STEPS:
-                products[step + 1] = multiply(step + 1)
+                products[step + 1] = multiply(step + 1, jobs)
+            else:
+                for job in jobs:
+                    job()
             combine(step, products.pop(step), o)
+            if rest is not None:
+                rest()
             if step + PREP_AHEAD < STEPS:
                 weights[step + PREP_AHEAD] = prepare(step + PREP_AHEAD)
 
@@ -173,15 +183,13 @@ def tile_eulerinteractionlayer_pa_kernel(
 
         with tc.tile_pool(name="head", bufs=1) as head:
             def load_rows(x):
-                tiles = []
+                raw = w_raw_pool.tile([P, 2, K], BF16, name="raw", tag="w_raw")
                 for bt in range(2):
-                    raw = head.tile([P, K], BF16, tag="raw", bufs=3)
                     nc.sync.dma_start(
-                        out=raw[:],
+                        out=raw[:, bt, :],
                         in_=x.rearrange("b f d -> b (f d)")[bt * P : (bt + 1) * P, :],
                     )
-                    tiles.append(raw)
-                return tiles
+                return raw
 
             raw_lam = load_rows(log_lam)
             polar_rows = head.tile([P, P], BF16)
@@ -210,6 +218,10 @@ def tile_eulerinteractionlayer_pa_kernel(
                     in_=vec.partition_broadcast(ROUND_FIELDS).unsqueeze(0),
                 )
 
+            for h in range(THIRDS):
+                load_third(0, h)
+            raw_x = [load_rows(r), load_rows(p)]
+
             nc.vector.tensor_copy(out=ident_bf[:], in_=ident[:])
 
             lam_rows = head.tile([P, P], F32)
@@ -218,18 +230,14 @@ def tile_eulerinteractionlayer_pa_kernel(
             nc.tensor.transpose(flipped[:], lam_rows[:], ident[:])
             nc.scalar.copy(out=lam_bias[:], in_=flipped[:, 32 : 32 + EMB])
 
-            raw_x = {}
-
             def quantise_rows(side, c0):
-                if c0 == 0:
-                    raw_x[side] = load_rows((r, p)[side])
                 samples = slice(side * BATCH, (side + 1) * BATCH)
                 tiles = []
                 for c in (c0, c0 + 1):
                     grouped = head.tile([P, BATCH, 4], BF16, align_bytes=64, bufs=2)
                     flipped = aux_pool.tile([P, 2, 2, P], F32, tag="aux")
                     for i in range(2):
-                        words = raw_x[side][i][:].bitcast(F32)
+                        words = raw_x[side][:, i, :].bitcast(F32)
                         for u in range(2):
                             nc.tensor.transpose(
                                 flipped[:, i, u, :],
@@ -251,13 +259,13 @@ def tile_eulerinteractionlayer_pa_kernel(
             def turn(raws):
                 tiles = []
                 for w0 in range(0, EMB // 2, 4):
-                    x_t = head.tile([P, 4, BATCH, 2], BF16, bufs=3)
+                    x_t = head.tile([P, 4, BATCH, 2], BF16, bufs=6)
                     x_t_words = x_t[:].bitcast(F32)
                     for bt in range(2):
                         by_word = head.tile([P, 4, FIELDS], F32, bufs=2)
                         nc.vector.tensor_copy(
                             out=by_word[:].rearrange("b w f -> b f w"),
-                            in_=raws[bt][:].bitcast(F32).rearrange("b (f w) -> b f w", w=EMB // 2)[
+                            in_=raws[:, bt, :].bitcast(F32).rearrange("b (f w) -> b f w", w=EMB // 2)[
                                 :, :, w0 : w0 + 4
                             ],
                         )
@@ -356,11 +364,13 @@ def tile_eulerinteractionlayer_pa_kernel(
                 if j == 2:
                     for step in range(PREP_AHEAD):
                         weights[step] = prepare(step)
-                    products[0] = multiply(0)
+                    products[0] = multiply(0, ())
                 if j > 2:
                     advance(j - 3, first_o)
 
-            mix(turn(raw_lam), False, finish_lam)
+            turned_lam = turn(raw_lam)
+            turned_theta = turn(raw_theta)
+            mix(turned_lam, False, finish_lam)
 
             nc.vector.tensor_copy(
                 out=shift_rows[:].rearrange("k j (g i) -> k j g i", i=VALS),
@@ -407,14 +417,15 @@ def tile_eulerinteractionlayer_pa_kernel(
                 op0=ALU.mult,
             )
 
-            mix(turn(raw_theta), True, finish_theta)
+            mix(turned_theta, True, finish_theta)
 
 
         with tc.tile_pool(name="tail", bufs=2) as tail:
 
             def group_sums(x, tiles):
                 sums = aux_pool.tile([P, tiles, P], F32, tag="aux", name="sums")
-                for m in range(tiles):
+
+                def add_tile(m):
                     for j in range(BLOCKS):
                         nc.tensor.matmul(
                             sums[:, m, :],
@@ -424,6 +435,10 @@ def tile_eulerinteractionlayer_pa_kernel(
                             start=(j == 0),
                             stop=(j == BLOCKS - 1),
                         )
+
+                return sums, [lambda m=m: add_tile(m) for m in range(tiles)]
+
+            def add_values(sums, tiles):
                 total = tail.tile([P, tiles * ROUND_FIELDS], F32, name="total")
                 nc.vector.tensor_reduce(
                     out=total[:],
@@ -463,137 +478,191 @@ def tile_eulerinteractionlayer_pa_kernel(
                     stop=(j == BLOCKS - 1),
                 )
 
-            def epilogue(rnd, o, first_side, sides, known_mean=None):
-                tiles = 2 * sides
-                samples = slice(first_side * BATCH, (first_side + sides) * BATCH)
-                state = {}
+            def centre_block(o, rnd, j, samples, mean):
+                nc.vector.scalar_tensor_tensor(
+                    out=o[:, j, samples],
+                    in0=o[:, j, samples],
+                    scalar=cols[:, j, ROW_CENTRED + rnd : ROW_CENTRED + rnd + 1],
+                    in1=mean,
+                    op0=ALU.add,
+                    op1=ALU.subtract,
+                )
 
-                def sum_values():
-                    state["wide"] = spread(group_sums(o[:, :, samples], tiles), tiles, ACT.Copy, 0.0)
+            def square_blocks(squares, o, j0, samples):
+                nc.scalar.activation(
+                    out=squares[:, j0 : j0 + 2, :],
+                    in_=o[:, j0 : j0 + 2, samples],
+                    func=ACT.Square,
+                )
 
-                def centre():
-                    if known_mean is None:
-                        mean = turn_back(state["wide"], tiles)
-                    else:
-                        mean = known_mean[:, samples]
-                        sums = [acc_pool.tile([P, P], F32, name="acc") for m in range(tiles)]
-                    squares = tail.tile([P, BLOCKS, sides * BATCH], F32, name="squares", bufs=1)
-                    for j in range(BLOCKS):
-                        nc.vector.scalar_tensor_tensor(
-                            out=o[:, j, samples],
-                            in0=o[:, j, samples],
-                            scalar=cols[:, j, ROW_CENTRED + rnd : ROW_CENTRED + rnd + 1],
-                            in1=mean,
-                            op0=ALU.add,
-                            op1=ALU.subtract,
+            def scale_block(o, j, side, rstd):
+                samples = slice(side * BATCH, (side + 1) * BATCH)
+                nc.vector.scalar_tensor_tensor(
+                    out=o[:, j, samples],
+                    in0=o[:, j, samples],
+                    scalar=cols[:, j, ROW_GAIN + side : ROW_GAIN + side + 1],
+                    in1=rstd,
+                    op0=ALU.mult,
+                    op1=ALU.mult,
+                )
+
+            def turn_out(turned, o, side, j0, by_product):
+                if by_product:
+                    row = ROW_SHIFT + side
+                    nc.tensor.matmul(
+                        turned[:],
+                        lhsT=ident_bf[:, row : row + 1].to_broadcast([P, P]),
+                        rhs=shift_rows[:, j0 : j0 + 2, :].unsqueeze(2).to_broadcast([P, 2, 2, P]),
+                        start=True,
+                        stop=False,
+                    )
+                for i in range(2):
+                    shift = cols[:, j0 + i, ROW_SHIFT + side : ROW_SHIFT + side + 1]
+                    for m in range(2):
+                        first = side * BATCH + m * P
+                        nc.tensor.matmul(
+                            turned[:, i, m, :],
+                            lhsT=o[:, j0 + i, first : first + P],
+                            rhs=ident[:],
+                            is_transpose=True,
+                            start=not by_product,
+                            stop=by_product and i == 1 and m == 1,
                         )
-                        if j % 2:
-                            nc.scalar.activation(
-                                out=squares[:, j - 1 : j + 1, :],
-                                in_=o[:, j - 1 : j + 1, samples],
-                                func=ACT.Square,
+                        if not by_product:
+                            nc.tensor.matmul(
+                                turned[:, i, m, :],
+                                lhsT=shift.to_broadcast([P, P]),
+                                rhs=ident[:],
+                                is_transpose=True,
+                                start=False,
+                                stop=True,
                             )
-                            if known_mean is not None:
-                                for i in (j - 1, j):
-                                    for m in range(tiles):
-                                        nc.tensor.matmul(
-                                            sums[m][:],
-                                            lhsT=squares[:, i, m * P : (m + 1) * P],
-                                            rhs=ident[:],
-                                            is_transpose=True,
-                                            start=(i == 0),
-                                            stop=(i == BLOCKS - 1),
-                                        )
-                    if known_mean is not None:
-                        total = tail.tile([P, tiles * ROUND_FIELDS], F32, name="total")
-                        for m in range(tiles):
-                            nc.vector.tensor_reduce(
-                                out=total[:, m * ROUND_FIELDS : (m + 1) * ROUND_FIELDS],
-                                in_=sums[m][:].rearrange("b (g i) -> b g i", i=VALS),
-                                axis=AXIS_X,
-                                op=ALU.add,
-                            )
-                        state["total"] = total
-                    state["squares"] = squares
 
-                def sum_squares():
-                    if known_mean is None:
-                        state["total"] = group_sums(state["squares"][:], tiles)
-                    state["wide"] = spread(
-                        state["total"],
-                        tiles,
-                        ACT.Abs_reciprocal_sqrt,
-                        eps[:, 0:1],
+            def copy_out(copy, y, turned, j0):
+                copy(
+                    out=y[:].rearrange("b m g (j i) -> b j (m g) i", i=VALS)[:, j0 : j0 + 2],
+                    in_=turned[:].rearrange("b j m (g i) -> b j (m g) i", i=VALS),
+                )
+
+            def store(y, rnd, side):
+                nc.sync.dma_start(
+                    out=outs[side].rearrange("(m b) f d -> b m (f d)", m=2)[
+                        :, :, rnd * ROUND_COLS : (rnd + 1) * ROUND_COLS
+                    ],
+                    in_=y[:].rearrange("b m g d -> b m (g d)"),
+                )
+
+            def stages(rnd, o):
+                both = slice(0, SAMPLES)
+                s = {}
+
+                def sum_jobs():
+                    s["sums"], jobs = group_sums(o[:], M_TILES)
+                    return jobs
+
+                def sum_rest():
+                    s["wide"] = spread(add_values(s["sums"], M_TILES), M_TILES, ACT.Copy, 0.0)
+
+                def back_jobs():
+                    def job():
+                        s["back"] = turn_back(s["wide"], M_TILES)
+
+                    return [job]
+
+                def centre_rest():
+                    s["squares"] = tail.tile([P, BLOCKS, SAMPLES], F32, name="squares", bufs=1)
+                    for j in range(BLOCKS):
+                        centre_block(o, rnd, j, both, s["back"])
+                        if j % 2:
+                            square_blocks(s["squares"], o, j - 1, both)
+
+                def square_jobs():
+                    s["sums"], jobs = group_sums(s["squares"][:], M_TILES)
+                    return jobs
+
+                def square_rest():
+                    s["wide"] = spread(
+                        add_values(s["sums"], M_TILES), M_TILES, ACT.Abs_reciprocal_sqrt, eps[:, 0:1]
                     )
 
-                def scale():
-                    rstd = turn_back(state["wide"], tiles)
-                    for side in range(first_side, first_side + sides):
+                def scale_rest():
+                    for side in range(SIDES):
                         for j in range(BLOCKS):
-                            first = (side - first_side) * BATCH
-                            nc.vector.scalar_tensor_tensor(
-                                out=o[:, j, side * BATCH : (side + 1) * BATCH],
-                                in0=o[:, j, side * BATCH : (side + 1) * BATCH],
-                                scalar=cols[:, j, ROW_GAIN + side : ROW_GAIN + side + 1],
-                                in1=rstd[:, first : first + BATCH],
-                                op0=ALU.mult,
-                                op1=ALU.mult,
-                            )
+                            scale_block(o, j, side, s["back"][:, side * BATCH : (side + 1) * BATCH])
 
-                def store(side):
+                def out_jobs(side):
+                    s["turned"] = {}
+
+                    def job(j0):
+                        turned = aux_pool.tile([P, 2, 2, P], F32, tag="aux", name="turned")
+                        turn_out(turned, o, side, j0, rnd >= 2)
+                        s["turned"][j0] = turned
+
+                    return [lambda j0=j0: job(j0) for j0 in range(0, BLOCKS, 2)]
+
+                def out_rest(side):
                     y = tail.tile([P, 2, ROUND_FIELDS, EMB], F32, name="y")
                     for j0 in range(0, BLOCKS, 2):
-                        turned = aux_pool.tile([P, 2, 2, P], F32, tag="aux")
-                        by_product = rnd >= 2
-                        if by_product:
-                            row = ROW_SHIFT + side
-                            nc.tensor.matmul(
-                                turned[:],
-                                lhsT=ident_bf[:, row : row + 1].to_broadcast([P, P]),
-                                rhs=shift_rows[:, j0 : j0 + 2, :]
-                                .unsqueeze(2)
-                                .to_broadcast([P, 2, 2, P]),
-                                start=True,
-                                stop=False,
-                            )
-                        for i in range(2):
-                            shift = cols[:, j0 + i, ROW_SHIFT + side : ROW_SHIFT + side + 1]
-                            for m in range(2):
-                                first = side * BATCH + m * P
-                                nc.tensor.matmul(
-                                    turned[:, i, m, :],
-                                    lhsT=o[:, j0 + i, first : first + P],
-                                    rhs=ident[:],
-                                    is_transpose=True,
-                                    start=not by_product,
-                                    stop=by_product and i == 1 and m == 1,
-                                )
-                                if not by_product:
+                        copy_out(nc.scalar.copy, y, s["turned"][j0], j0)
+                    store(y, rnd, side)
+
+                return [
+                    (sum_jobs, sum_rest),
+                    (back_jobs, centre_rest),
+                    (square_jobs, square_rest),
+                    (back_jobs, scale_rest),
+                    (lambda: out_jobs(0), lambda: out_rest(0)),
+                    (lambda: out_jobs(1), lambda: out_rest(1)),
+                ]
+
+            def last_stages(rnd, side, o, mean):
+                samples = slice(side * BATCH, (side + 1) * BATCH)
+                s = {}
+
+                def centre():
+                    squares = tail.tile([P, BLOCKS, BATCH], F32, name="squares", bufs=1)
+                    sums = [acc_pool.tile([P, P], F32, name="acc") for m in range(2)]
+                    for j in range(BLOCKS):
+                        centre_block(o, rnd, j, samples, mean[:, samples])
+                        if j % 2:
+                            square_blocks(squares, o, j - 1, samples)
+                            for i in (j - 1, j):
+                                for m in range(2):
                                     nc.tensor.matmul(
-                                        turned[:, i, m, :],
-                                        lhsT=shift.to_broadcast([P, P]),
+                                        sums[m][:],
+                                        lhsT=squares[:, i, m * P : (m + 1) * P],
                                         rhs=ident[:],
                                         is_transpose=True,
-                                        start=False,
-                                        stop=True,
+                                        start=(i == 0),
+                                        stop=(i == BLOCKS - 1),
                                     )
-                        copy = nc.vector.tensor_copy if known_mean is not None and j0 == 2 else nc.scalar.copy
-                        copy(
-                            out=y[:]
-                            .rearrange("b m g (j i) -> b j (m g) i", i=VALS)[:, j0 : j0 + 2],
-                            in_=turned[:].rearrange("b j m (g i) -> b j (m g) i", i=VALS),
+                    s["total"] = tail.tile([P, 2 * ROUND_FIELDS], F32, name="total")
+                    for m in range(2):
+                        nc.vector.tensor_reduce(
+                            out=s["total"][:, m * ROUND_FIELDS : (m + 1) * ROUND_FIELDS],
+                            in_=sums[m][:].rearrange("b (g i) -> b g i", i=VALS),
+                            axis=AXIS_X,
+                            op=ALU.add,
                         )
-                    nc.sync.dma_start(
-                        out=outs[side].rearrange("(m b) f d -> b m (f d)", m=2)[
-                            :, :, rnd * ROUND_COLS : (rnd + 1) * ROUND_COLS
-                        ],
-                        in_=y[:].rearrange("b m g d -> b m (g d)"),
-                    )
 
-                stores = [lambda side=side: store(side) for side in range(first_side, first_side + sides)]
-                if known_mean is None:
-                    return [sum_values, centre, sum_squares, scale] + stores
-                return [centre, sum_squares, scale] + stores
+                def spread_out():
+                    s["wide"] = spread(s["total"], 2, ACT.Abs_reciprocal_sqrt, eps[:, 0:1])
+
+                def scale():
+                    rstd = turn_back(s["wide"], 2)
+                    for j in range(BLOCKS):
+                        scale_block(o, j, side, rstd)
+
+                def finish():
+                    y = tail.tile([P, 2, ROUND_FIELDS, EMB], F32, name="y")
+                    for j0 in range(0, BLOCKS, 2):
+                        turned = aux_pool.tile([P, 2, 2, P], F32, tag="aux", name="turned")
+                        turn_out(turned, o, side, j0, True)
+                        copy = nc.vector.tensor_copy if j0 == 2 else nc.scalar.copy
+                        copy_out(copy, y, turned, j0)
+                    store(y, rnd, side)
+
+                return centre, spread_out, scale, finish
 
             pending = []
             o = first_o
@@ -601,6 +670,7 @@ def tile_eulerinteractionlayer_pa_kernel(
             for step in range(HEAD_ADVANCE, STEPS):
                 rnd, j = divmod(step, BLOCKS)
                 if j == 0:
+                    pending = stages(rnd - 1, o)
                     o = (tail if rnd % 2 else o_pool).tile([P, BLOCKS, SAMPLES], F32, name="o", bufs=1)
                 if rnd == ROUNDS - 1:
                     if j == 0:
@@ -608,18 +678,11 @@ def tile_eulerinteractionlayer_pa_kernel(
                     else:
                         add_to_mean(mean, o, j - 1)
                 if pending:
-                    pending.pop(0)()
-                advance(step, o)
-                if j == BLOCKS - 1:
-                    pending = epilogue(rnd, o, 0, SIDES)
-                    if rnd == ROUNDS - 1:
-                        add_to_mean(mean, o, j)
-                        pending = [
-                            work
-                            for pair in zip(
-                                epilogue(rnd, o, 0, 1, mean), epilogue(rnd, o, 1, 1, mean)
-                            )
-                            for work in pair
-                        ]
-            for work in pending:
-                work()
+                    get_jobs, rest = pending[j]
+                    advance(step, o, get_jobs(), rest)
+                else:
+                    advance(step, o)
+            add_to_mean(mean, o, BLOCKS - 1)
+            for pair in zip(*[last_stages(ROUNDS - 1, side, o, mean) for side in range(SIDES)]):
+                for work in pair:
+                    work()

import math

import concourse.mybir as mybir
from concourse.masks import make_identity

F32 = mybir.dt.float32
BF16 = mybir.dt.bfloat16
I32 = mybir.dt.int32
U32 = mybir.dt.uint32
U8 = mybir.dt.uint8
FP8X4 = mybir.dt.float8_e4m3fn_x4
ACT = mybir.ActivationFunctionType
ALU = mybir.AluOpType
AXIS_X = mybir.AxisListType.X

P = 128
BATCH = 256
FIELDS = 128
EMB = 24
K = FIELDS * EMB
SIDES = 2
M_TILES = 4
SAMPLES = SIDES * BATCH
K_PASS = 512
PASSES = K // K_PASS
HALF = K_PASS // 2
ROUND_FIELDS = 32
ROUND_COLS = ROUND_FIELDS * EMB
ROUNDS = FIELDS // ROUND_FIELDS
VALS = 4
BLOCKS = EMB // VALS
STEPS = ROUNDS * BLOCKS
THIRD = 2
THIRDS = PASSES // THIRD
LN_EPS = 1e-5
HEAD_ADVANCE = 3
PREP_AHEAD = 2
HEAD_STEPS = 1
ROW_BIAS = 0
ROW_CENTRED = 32
ROW_GAIN = 64
ROW_SHIFT = 66

FLOPS = 2 * (2 * BATCH) * K * K + 2 * 2 * BATCH * EMB * FIELDS * FIELDS


def tile_eulerinteractionlayer_pa_kernel(
    tc,
    r,
    p,
    log_lam,
    theta,
    inter_orders,
    im_w,
    im_b,
    bias_lam,
    bias_theta,
    norm_r_w,
    norm_r_b,
    norm_p_w,
    norm_p_b,
    out_0,
    out_1,
):
    nc = tc.nc
    outs = (out_0, out_1)
    flat = [o.rearrange("b f d -> (b f d)") for o in outs]
    park = [x.rearrange("(j g n) -> j g n", j=BLOCKS, g=FIELDS) for x in flat]
    unpark = [x.rearrange("(j r q b) -> j q r b", j=BLOCKS, r=ROUNDS, q=P) for x in flat]
    with (
        tc.tile_pool(name="keep", bufs=1) as keep,
        tc.tile_pool(name="w_raw", bufs=2 * THIRDS) as w_raw_pool,
        tc.tile_pool(name="w_grouped", bufs=2) as w_grouped_pool,
        tc.tile_pool(name="w_mx", bufs=PREP_AHEAD + 1) as w_mx_pool,
        tc.tile_pool(name="o", bufs=1) as o_pool,
        tc.psum_pool(name="acc", bufs=3) as acc_pool,
        tc.psum_pool(name="aux", bufs=5) as aux_pool,
    ):
        ident = keep.tile([P, P], F32)
        make_identity(nc, ident[:])
        eps = keep.tile([P, 1], F32)
        nc.vector.memset(eps[:], LN_EPS)
        orders = keep.tile([P, FIELDS], BF16)
        nc.sync.dma_start(out=orders[:], in_=inter_orders)

        a_codes = keep.tile([P, PASSES, SAMPLES], U32, align_bytes=64)
        a_scales = keep.tile([P, PASSES, SAMPLES], U8, align_bytes=64)
        neg_polar = keep.tile([P, BLOCKS, ROUNDS, SAMPLES], F32)
        cols = keep.tile([P, BLOCKS, 68], F32)
        neg_bias = keep.tile([P, BLOCKS, ROUNDS], F32)
        ident_bf = keep.tile([P, P], BF16)
        shift_rows = keep.tile([P, BLOCKS, P], BF16)
        lam_bias = keep.tile([P, EMB], F32)
        mean_block = keep.tile([P, P], F32)

        w_raw = {}

        def load_third(rnd, h):
            tile = w_raw_pool.tile([P, THIRD, 4, ROUND_COLS], BF16, name="w_third", tag="w_raw")
            for i in range(THIRD):
                first = (h * THIRD + i) * K_PASS
                nc.sync.dma_start(
                    out=tile[:, i, :, :],
                    in_=im_w[
                        first : first + K_PASS, rnd * ROUND_COLS : (rnd + 1) * ROUND_COLS
                    ].rearrange("(q t) n -> q t n", t=4),
                )
            w_raw[rnd, h] = tile

        def prepare(step):
            rnd, j = divmod(step, BLOCKS)
            grouped = w_grouped_pool.tile([P, PASSES, P, 4], BF16, align_bytes=64)
            for h in range(THIRDS):
                if j == 0 and rnd:
                    load_third(rnd, h)
                on_vector = step < HEAD_STEPS or (step * THIRDS + h) % 3 == 0
                regroup = nc.vector.tensor_copy if on_vector else nc.scalar.copy
                regroup(
                    out=grouped[:, h * THIRD : (h + 1) * THIRD, :, :].rearrange(
                        "q c (g i) t -> q c g t i", i=VALS
                    ),
                    in_=w_raw[rnd, h][:].rearrange("q c t (g j i) -> q j c g t i", j=BLOCKS, i=VALS)[
                        :, j
                    ],
                )
            codes = w_mx_pool.tile([P, PASSES, P], U32, align_bytes=64)
            scales = w_mx_pool.tile([P, PASSES, P], U8, align_bytes=64)
            for lo, hi in ((0, 4), (4, 6)):
                nc.vector.quantize_mx(
                    out=codes[:, lo:hi, :].rearrange("q c n -> q (c n)").bitcast(FP8X4),
                    scales=scales[:, lo:hi, :].rearrange("q c n -> q (c n)"),
                    in_=grouped[:, lo:hi, :, :].rearrange("q c n t -> q (c n t)"),
                )
            return codes, scales

        def multiply(step, jobs):
            codes, scales = weights[step]
            acc = acc_pool.tile([P, SAMPLES], F32, name="acc")
            slots = PASSES // 2
            for c in range(PASSES):
                nc.tensor.matmul_mx(
                    out=acc[:],
                    lhsT=codes[:, c, :].bitcast(FP8X4),
                    lhsT_scale=scales[:, c, :],
                    rhs=a_codes[:, c, :].bitcast(FP8X4),
                    rhs_scale=a_scales[:, c, :],
                    start=(c == 0),
                    stop=(c == PASSES - 1),
                )
                if c % 2:
                    slot = c // 2
                    for job in jobs[slot * len(jobs) // slots : (slot + 1) * len(jobs) // slots]:
                        job()
            return acc

        def combine(step, acc, o):
            rnd, j = divmod(step, BLOCKS)
            nc.vector.scalar_tensor_tensor(
                out=o[:, j, :],
                in0=acc[:],
                scalar=neg_bias[:, j, rnd : rnd + 1],
                in1=neg_polar[:, j, rnd, :],
                op0=ALU.max,
                op1=ALU.subtract,
            )

        weights = {}
        products = {}

        def advance(step, o, jobs=(), rest=None):
            if step + 1 < STEPS:
                products[step + 1] = multiply(step + 1, jobs)
            else:
                for job in jobs:
                    job()
            combine(step, products.pop(step), o)
            if rest is not None:
                rest()
            if step + PREP_AHEAD < STEPS:
                weights[step + PREP_AHEAD] = prepare(step + PREP_AHEAD)

        first_o = o_pool.tile([P, BLOCKS, SAMPLES], F32, name="o")

        with tc.tile_pool(name="head", bufs=1) as head:
            def load_rows(x):
                raw = w_raw_pool.tile([P, 2, K], BF16, name="raw", tag="w_raw")
                for bt in range(2):
                    nc.sync.dma_start(
                        out=raw[:, bt, :],
                        in_=x.rearrange("b f d -> b (f d)")[bt * P : (bt + 1) * P, :],
                    )
                return raw

            raw_lam = load_rows(log_lam)
            polar_rows = head.tile([P, P], BF16)
            nc.gpsimd.memset(polar_rows[:], 0.0)
            nc.sync.dma_start(out=polar_rows[0:EMB, :], in_=bias_theta.rearrange("o d g -> (o d) g"))
            nc.sync.dma_start(
                out=polar_rows[32 : 32 + EMB, :], in_=bias_lam.rearrange("o d g -> (o d) g")
            )

            raw_theta = load_rows(theta)
            rows = head.tile([P, ROUND_FIELDS, EMB], BF16)
            nc.gpsimd.memset(rows[:], 0.0)
            for first in (ROW_BIAS, ROW_CENTRED):
                nc.sync.dma_start(
                    out=rows[first : first + ROUNDS, :, :],
                    in_=im_b.rearrange("(r g d) -> r g d", r=ROUNDS, g=ROUND_FIELDS),
                )
            for row, vec in (
                (ROW_GAIN, norm_r_w),
                (ROW_GAIN + 1, norm_p_w),
                (ROW_SHIFT, norm_r_b),
                (ROW_SHIFT + 1, norm_p_b),
            ):
                nc.sync.dma_start(
                    out=rows[row : row + 1, :, :],
                    in_=vec.partition_broadcast(ROUND_FIELDS).unsqueeze(0),
                )

            for h in range(THIRDS):
                load_third(0, h)
            raw_x = [load_rows(r), load_rows(p)]

            nc.vector.tensor_copy(out=ident_bf[:], in_=ident[:])

            lam_rows = head.tile([P, P], F32)
            nc.vector.tensor_copy(out=lam_rows[:], in_=polar_rows[:])
            flipped = aux_pool.tile([P, P], F32, tag="aux")
            nc.tensor.transpose(flipped[:], lam_rows[:], ident[:])
            nc.scalar.copy(out=lam_bias[:], in_=flipped[:, 32 : 32 + EMB])

            def quantise_rows(side, c0):
                samples = slice(side * BATCH, (side + 1) * BATCH)
                tiles = []
                for c in (c0, c0 + 1):
                    grouped = head.tile([P, BATCH, 4], BF16, align_bytes=64, bufs=2)
                    flipped = aux_pool.tile([P, 2, 2, P], F32, tag="aux")
                    for i in range(2):
                        words = raw_x[side][:, i, :].bitcast(F32)
                        for u in range(2):
                            nc.tensor.transpose(
                                flipped[:, i, u, :],
                                words[:, c * HALF + u : (c + 1) * HALF : 2],
                                ident[:],
                            )
                    nc.scalar.copy(
                        out=grouped[:].bitcast(F32).rearrange("q (i b) u -> q i b u", i=2),
                        in_=flipped[:].rearrange("q i u b -> q i b u"),
                    )
                    tiles.append(grouped)
                for c, grouped in zip((c0, c0 + 1), tiles):
                    nc.vector.quantize_mx(
                        out=a_codes[:, c, samples].bitcast(FP8X4),
                        scales=a_scales[:, c, samples],
                        in_=grouped[:].rearrange("q n t -> q (n t)"),
                    )

            def turn(raws):
                tiles = []
                for w0 in range(0, EMB // 2, 4):
                    x_t = head.tile([P, 4, BATCH, 2], BF16, bufs=6)
                    x_t_words = x_t[:].bitcast(F32)
                    for bt in range(2):
                        by_word = head.tile([P, 4, FIELDS], F32, bufs=2)
                        nc.vector.tensor_copy(
                            out=by_word[:].rearrange("b w f -> b f w"),
                            in_=raws[:, bt, :].bitcast(F32).rearrange("b (f w) -> b f w", w=EMB // 2)[
                                :, :, w0 : w0 + 4
                            ],
                        )
                        flipped = aux_pool.tile([P, 4, P], F32, tag="aux")
                        for i in range(4):
                            nc.tensor.transpose(flipped[:, i, :], by_word[:, i, :], ident[:])
                        nc.scalar.copy(
                            out=x_t_words[:, :, bt * P : (bt + 1) * P, 0], in_=flipped[:]
                        )
                    tiles.append(x_t)
                return tiles

            def mix(tiles, add_bias, finish):
                pair = []
                for w0, x_t in zip(range(0, EMB // 2, 4), tiles):
                    for i in range(4):
                        mixed = aux_pool.tile([P, BATCH, 2], F32, tag="aux")
                        if add_bias:
                            row = 2 * (w0 + i)
                            nc.tensor.matmul(
                                mixed[:],
                                lhsT=polar_rows[:],
                                rhs=ident_bf[:, row : row + 2]
                                .unsqueeze(1)
                                .to_broadcast([P, BATCH, 2]),
                                start=True,
                                stop=False,
                            )
                        nc.tensor.matmul(
                            mixed[:].rearrange("g b e -> g (b e)"),
                            lhsT=orders[:],
                            rhs=x_t[:, i, :, :].rearrange("f b e -> f (b e)"),
                            start=not add_bias,
                            stop=True,
                        )
                        pair.append(mixed[:].rearrange("g b e -> g e b"))
                        if i % 2:
                            finish((w0 + i) // 2, pair)
                            pair = []

            held = neg_polar[:].rearrange("g j r s -> g j (r s)").rearrange(
                "g j (t i b) -> g j t i b", t=2, i=VALS
            )

            def finish_lam(j, pair):
                for i in range(VALS):
                    nc.scalar.activation(
                        out=held[:, j, 0, i, :],
                        in_=pair[i // 2][:, i % 2, :],
                        func=ACT.Exp,
                        bias=lam_bias[:, j * VALS + i : j * VALS + i + 1],
                    )

            def finish_theta(j, pair):
                block_angle = head.tile([P, VALS, BATCH], F32, name="angle", bufs=2)
                turns = []
                for mixed in pair:
                    whole = head.tile([P, 2, BATCH], I32, name="whole", bufs=2)
                    nc.vector.tensor_scalar(
                        out=whole[:],
                        in0=mixed,
                        scalar1=1.0 / (2.0 * math.pi),
                        scalar2=None,
                        op0=ALU.mult,
                    )
                    turns.append(whole)
                for i, mixed in enumerate(pair):
                    nc.vector.scalar_tensor_tensor(
                        out=block_angle[:, 2 * i : 2 * i + 2, :],
                        in0=mixed,
                        scalar=1.0 / (2.0 * math.pi),
                        in1=turns[i][:],
                        op0=ALU.mult,
                        op1=ALU.subtract,
                    )
                angle = block_angle[:].rearrange("g i b -> g (i b)")
                lam = held[:, j, 0, :, :].rearrange("g i b -> g (i b)")
                neg_sin = head.tile([P, VALS * BATCH], F32, bufs=2)
                nc.scalar.activation(out=neg_sin[:], in_=angle, func=ACT.Sin, scale=-2.0 * math.pi)
                nc.scalar.activation(out=angle, in_=angle, func=ACT.Sin, scale=math.pi)
                nc.scalar.activation(out=angle, in_=angle, func=ACT.Square, scale=math.sqrt(2.0))
                nc.vector.tensor_tensor(out=neg_sin[:], in0=neg_sin[:], in1=lam, op=ALU.mult)
                nc.vector.scalar_tensor_tensor(
                    out=angle, in0=angle, scalar=1.0, in1=lam, op0=ALU.subtract, op1=ALU.mult
                )
                for side, term in ((0, angle), (1, neg_sin[:])):
                    nc.sync.dma_start(out=park[side][j], in_=term)
                for side in range(SIDES):
                    nc.sync.dma_start(
                        out=neg_polar[:, j, :, side * BATCH : (side + 1) * BATCH],
                        in_=unpark[side][j],
                    )
                if j < 3:
                    for unit in (4 * j, 4 * j + 2):
                        quantise_rows(*divmod(unit, PASSES))
                if j == 2:
                    for step in range(PREP_AHEAD):
                        weights[step] = prepare(step)
                    products[0] = multiply(0, ())
                if j > 2:
                    advance(j - 3, first_o)

            turned_lam = turn(raw_lam)
            turned_theta = turn(raw_theta)
            mix(turned_lam, False, finish_lam)

            nc.vector.tensor_copy(
                out=shift_rows[:].rearrange("k j (g i) -> k j g i", i=VALS),
                in_=rows[:].rearrange("k g (j i) -> k j g i", j=BLOCKS),
            )
            rows_f32 = head.tile([P, BLOCKS, P], F32)
            nc.vector.tensor_copy(out=rows_f32[:], in_=shift_rows[:])
            field_sum = head.tile([P, ROUND_FIELDS], F32)
            nc.vector.tensor_reduce(out=field_sum[:], in_=rows[:], axis=AXIS_X, op=ALU.add)
            centred_rows = rows_f32[32:64, :, :].rearrange("k j (g i) -> k j g i", i=VALS)
            for j in range(BLOCKS):
                nc.vector.scalar_tensor_tensor(
                    out=centred_rows[:, j],
                    in0=field_sum[32:64, :].unsqueeze(2).to_broadcast([32, ROUND_FIELDS, VALS]),
                    scalar=-1.0 / EMB,
                    in1=centred_rows[:, j],
                    op0=ALU.mult,
                    op1=ALU.add,
                )
            for j0 in range(0, BLOCKS, 3):
                flipped = aux_pool.tile([P, 3, P], F32, tag="aux")
                for i in range(3):
                    nc.tensor.transpose(flipped[:, i, :], rows_f32[:, j0 + i, :], ident[:])
                nc.scalar.copy(out=cols[:, j0 : j0 + 3, :], in_=flipped[:, :, 0:68])
            same_field = head.tile([P, ROUND_FIELDS], F32)
            nc.vector.tensor_reduce(
                out=same_field[:],
                in_=ident[:].rearrange("q (g i) -> q g i", i=VALS),
                axis=AXIS_X,
                op=ALU.add,
            )
            nc.vector.tensor_scalar(
                out=mean_block[:].rearrange("q (g i) -> q g i", i=VALS),
                in0=same_field[:].unsqueeze(2).to_broadcast([P, ROUND_FIELDS, VALS]),
                scalar1=1.0 / EMB,
                scalar2=None,
                op0=ALU.mult,
            )
            nc.vector.tensor_scalar(
                out=neg_bias[:],
                in0=cols[:, :, ROW_BIAS : ROW_BIAS + ROUNDS],
                scalar1=-1.0,
                scalar2=None,
                op0=ALU.mult,
            )

            mix(turned_theta, True, finish_theta)


        with tc.tile_pool(name="tail", bufs=2) as tail:

            def group_sums(x, tiles):
                sums = aux_pool.tile([P, tiles, P], F32, tag="aux", name="sums")

                def add_tile(m):
                    for j in range(BLOCKS):
                        nc.tensor.matmul(
                            sums[:, m, :],
                            lhsT=x[:, j, m * P : (m + 1) * P],
                            rhs=ident[:],
                            is_transpose=True,
                            start=(j == 0),
                            stop=(j == BLOCKS - 1),
                        )

                return sums, [lambda m=m: add_tile(m) for m in range(tiles)]

            def add_values(sums, tiles):
                total = tail.tile([P, tiles * ROUND_FIELDS], F32, name="total")
                nc.vector.tensor_reduce(
                    out=total[:],
                    in_=sums[:].rearrange("b m (g i) -> b (m g) i", i=VALS),
                    axis=AXIS_X,
                    op=ALU.add,
                )
                return total

            def spread(total, tiles, func, bias):
                wide = tail.tile([P, tiles * ROUND_FIELDS, VALS], F32, name="wide")
                nc.scalar.activation(
                    out=wide[:],
                    in_=total[:].unsqueeze(2).to_broadcast([P, tiles * ROUND_FIELDS, VALS]),
                    func=func,
                    scale=1.0 / EMB,
                    bias=bias,
                )
                return wide

            def turn_back(wide, tiles):
                back = aux_pool.tile([P, tiles, P], F32, tag="aux", name="back")
                for m in range(tiles):
                    nc.tensor.transpose(
                        back[:, m, :],
                        wide[:].rearrange("b (m g) i -> b m (g i)", m=tiles)[:, m, :],
                        ident[:],
                    )
                return back[:].rearrange("q m b -> q (m b)")

            def add_to_mean(mean, o, j):
                nc.tensor.matmul(
                    mean[:],
                    lhsT=mean_block[:],
                    rhs=o[:, j, :],
                    start=(j == 0),
                    stop=(j == BLOCKS - 1),
                )

            def centre_block(o, rnd, j, samples, mean):
                nc.vector.scalar_tensor_tensor(
                    out=o[:, j, samples],
                    in0=o[:, j, samples],
                    scalar=cols[:, j, ROW_CENTRED + rnd : ROW_CENTRED + rnd + 1],
                    in1=mean,
                    op0=ALU.add,
                    op1=ALU.subtract,
                )

            def square_blocks(squares, o, j0, samples):
                nc.scalar.activation(
                    out=squares[:, j0 : j0 + 2, :],
                    in_=o[:, j0 : j0 + 2, samples],
                    func=ACT.Square,
                )

            def scale_block(o, j, side, rstd):
                samples = slice(side * BATCH, (side + 1) * BATCH)
                nc.vector.scalar_tensor_tensor(
                    out=o[:, j, samples],
                    in0=o[:, j, samples],
                    scalar=cols[:, j, ROW_GAIN + side : ROW_GAIN + side + 1],
                    in1=rstd,
                    op0=ALU.mult,
                    op1=ALU.mult,
                )

            def turn_out(turned, o, side, j0, by_product):
                if by_product:
                    row = ROW_SHIFT + side
                    nc.tensor.matmul(
                        turned[:],
                        lhsT=ident_bf[:, row : row + 1].to_broadcast([P, P]),
                        rhs=shift_rows[:, j0 : j0 + 2, :].unsqueeze(2).to_broadcast([P, 2, 2, P]),
                        start=True,
                        stop=False,
                    )
                for i in range(2):
                    shift = cols[:, j0 + i, ROW_SHIFT + side : ROW_SHIFT + side + 1]
                    for m in range(2):
                        first = side * BATCH + m * P
                        nc.tensor.matmul(
                            turned[:, i, m, :],
                            lhsT=o[:, j0 + i, first : first + P],
                            rhs=ident[:],
                            is_transpose=True,
                            start=not by_product,
                            stop=by_product and i == 1 and m == 1,
                        )
                        if not by_product:
                            nc.tensor.matmul(
                                turned[:, i, m, :],
                                lhsT=shift.to_broadcast([P, P]),
                                rhs=ident[:],
                                is_transpose=True,
                                start=False,
                                stop=True,
                            )

            def copy_out(copy, y, turned, j0):
                copy(
                    out=y[:].rearrange("b m g (j i) -> b j (m g) i", i=VALS)[:, j0 : j0 + 2],
                    in_=turned[:].rearrange("b j m (g i) -> b j (m g) i", i=VALS),
                )

            def store(y, rnd, side):
                nc.sync.dma_start(
                    out=outs[side].rearrange("(m b) f d -> b m (f d)", m=2)[
                        :, :, rnd * ROUND_COLS : (rnd + 1) * ROUND_COLS
                    ],
                    in_=y[:].rearrange("b m g d -> b m (g d)"),
                )

            def stages(rnd, o):
                both = slice(0, SAMPLES)
                s = {}

                def sum_jobs():
                    s["sums"], jobs = group_sums(o[:], M_TILES)
                    return jobs

                def sum_rest():
                    s["wide"] = spread(add_values(s["sums"], M_TILES), M_TILES, ACT.Copy, 0.0)

                def back_jobs():
                    def job():
                        s["back"] = turn_back(s["wide"], M_TILES)

                    return [job]

                def centre_rest():
                    s["squares"] = tail.tile([P, BLOCKS, SAMPLES], F32, name="squares", bufs=1)
                    for j in range(BLOCKS):
                        centre_block(o, rnd, j, both, s["back"])
                        if j % 2:
                            square_blocks(s["squares"], o, j - 1, both)

                def square_jobs():
                    s["sums"], jobs = group_sums(s["squares"][:], M_TILES)
                    return jobs

                def square_rest():
                    s["wide"] = spread(
                        add_values(s["sums"], M_TILES), M_TILES, ACT.Abs_reciprocal_sqrt, eps[:, 0:1]
                    )

                def scale_rest():
                    for side in range(SIDES):
                        for j in range(BLOCKS):
                            scale_block(o, j, side, s["back"][:, side * BATCH : (side + 1) * BATCH])

                def out_jobs(side):
                    s["turned"] = {}

                    def job(j0):
                        turned = aux_pool.tile([P, 2, 2, P], F32, tag="aux", name="turned")
                        turn_out(turned, o, side, j0, rnd >= 2)
                        s["turned"][j0] = turned

                    return [lambda j0=j0: job(j0) for j0 in range(0, BLOCKS, 2)]

                def out_rest(side):
                    y = tail.tile([P, 2, ROUND_FIELDS, EMB], F32, name="y")
                    for j0 in range(0, BLOCKS, 2):
                        copy_out(nc.scalar.copy, y, s["turned"][j0], j0)
                    store(y, rnd, side)

                return [
                    (sum_jobs, sum_rest),
                    (back_jobs, centre_rest),
                    (square_jobs, square_rest),
                    (back_jobs, scale_rest),
                    (lambda: out_jobs(0), lambda: out_rest(0)),
                    (lambda: out_jobs(1), lambda: out_rest(1)),
                ]

            def last_stages(rnd, side, o, mean):
                samples = slice(side * BATCH, (side + 1) * BATCH)
                s = {}

                def centre():
                    squares = tail.tile([P, BLOCKS, BATCH], F32, name="squares", bufs=1)
                    sums = [acc_pool.tile([P, P], F32, name="acc") for m in range(2)]
                    for j in range(BLOCKS):
                        centre_block(o, rnd, j, samples, mean[:, samples])
                        if j % 2:
                            square_blocks(squares, o, j - 1, samples)
                            for i in (j - 1, j):
                                for m in range(2):
                                    nc.tensor.matmul(
                                        sums[m][:],
                                        lhsT=squares[:, i, m * P : (m + 1) * P],
                                        rhs=ident[:],
                                        is_transpose=True,
                                        start=(i == 0),
                                        stop=(i == BLOCKS - 1),
                                    )
                    s["total"] = tail.tile([P, 2 * ROUND_FIELDS], F32, name="total")
                    for m in range(2):
                        nc.vector.tensor_reduce(
                            out=s["total"][:, m * ROUND_FIELDS : (m + 1) * ROUND_FIELDS],
                            in_=sums[m][:].rearrange("b (g i) -> b g i", i=VALS),
                            axis=AXIS_X,
                            op=ALU.add,
                        )

                def spread_out():
                    s["wide"] = spread(s["total"], 2, ACT.Abs_reciprocal_sqrt, eps[:, 0:1])

                def scale():
                    rstd = turn_back(s["wide"], 2)
                    for j in range(BLOCKS):
                        scale_block(o, j, side, rstd)

                def finish():
                    y = tail.tile([P, 2, ROUND_FIELDS, EMB], F32, name="y")
                    for j0 in range(0, BLOCKS, 2):
                        turned = aux_pool.tile([P, 2, 2, P], F32, tag="aux", name="turned")
                        turn_out(turned, o, side, j0, True)
                        copy = nc.vector.tensor_copy if j0 == 2 else nc.scalar.copy
                        copy_out(copy, y, turned, j0)
                    store(y, rnd, side)

                return centre, spread_out, scale, finish

            pending = []
            o = first_o
            mean = None
            for step in range(HEAD_ADVANCE, STEPS):
                rnd, j = divmod(step, BLOCKS)
                if j == 0:
                    pending = stages(rnd - 1, o)
                    o = (tail if rnd % 2 else o_pool).tile([P, BLOCKS, SAMPLES], F32, name="o", bufs=1)
                if rnd == ROUNDS - 1:
                    if j == 0:
                        mean = aux_pool.tile([P, SAMPLES], F32, tag="aux", name="mean")
                    else:
                        add_to_mean(mean, o, j - 1)
                if pending:
                    get_jobs, rest = pending[j]
                    advance(step, o, get_jobs(), rest)
                else:
                    advance(step, o)
            add_to_mean(mean, o, BLOCKS - 1)
            for pair in zip(*[last_stages(ROUNDS - 1, side, o, mean) for side in range(SIDES)]):
                for work in pair:
                    work()
